import numpy as np
import ml_dtypes


def mxq(x, axis, fmt="e4m3"):
    dtype, down = {"e4m3": (ml_dtypes.float8_e4m3fn, 7), "e5m2": (ml_dtypes.float8_e5m2, 14)}[fmt]
    v = np.moveaxis(np.asarray(x, np.float32).astype(ml_dtypes.bfloat16).astype(np.float64), axis, -1)
    blocks = v.reshape(v.shape[:-1] + (-1, 32))
    amax = np.abs(blocks).max(-1, keepdims=True)
    byte = np.maximum(np.where(amax > 0, np.frexp(amax)[1] - 1 + 127, 0) - down, 1)
    scale = np.exp2(byte - 127.0)
    codes = (blocks / scale).astype(np.float32).astype(dtype).astype(np.float64)
    return np.moveaxis((codes * scale).reshape(v.shape), -1, axis)


WIDE = False


def mx_kscale(k):
    if not WIDE:
        return np.ones(k)
    levels = np.array([10, -10, 5, -5, 0])
    a = np.random.permutation(np.resize(levels, k // 512 * 4)).reshape(k // 512, 4)
    idx = np.arange(k)
    return np.exp2(a[idx // 512, idx % 128 // 32])


BF16 = ml_dtypes.bfloat16


def bf(x):
    return np.asarray(x, np.float32).astype(BF16)


def f64(x):
    return np.asarray(x).astype(np.float64)


E2M1 = np.array([0.0, 0.5, 1.0, 1.5, 2.0, 3.0, 4.0, 6.0, -0.0, -0.5, -1.0, -1.5, -2.0, -3.0, -4.0, -6.0])


def pack_weight(w, fmt):
    k, n = w.shape
    w = f64(bf(w)).reshape(k // 32, 32, n)
    amax = np.abs(w).max(1)
    if fmt == "e4m3":
        byte = np.frexp(amax)[1] - 1 + 127 - 7
    else:
        mant, ex = np.frexp(amax / 6.0)
        byte = np.where(mant > 0.5, ex, ex - 1) + 127
    byte = np.clip(np.where(amax > 0, byte, 1), 1, 254)
    scaled = (w * np.exp2(127.0 - byte)[:, None, :]).reshape(k, n).astype(np.float32)
    by_word = np.ascontiguousarray(scaled.reshape(k // 512, 128, 4, n).transpose(0, 1, 3, 2))
    if fmt == "e4m3":
        words = by_word.astype(ml_dtypes.float8_e4m3fn).view(np.uint8)
    else:
        c = by_word.astype(ml_dtypes.float4_e2m1fn).view(np.uint8) & 0xF
        words = c[..., 0::2] | (c[..., 1::2] << 4)
    return np.ascontiguousarray(words), np.ascontiguousarray(byte.astype(np.uint8).reshape(k // 512, 16, n))


def unpack_weight(words, scales, fmt):
    g, p, n, _ = words.shape
    if fmt == "e4m3":
        vals = np.ascontiguousarray(words).view(ml_dtypes.float8_e4m3fn).astype(np.float64)
    else:
        nib = np.empty((g, p, n, 4), np.uint8)
        nib[..., 0::2] = words & 0xF
        nib[..., 1::2] = words >> 4
        vals = E2M1[nib]
    vals = vals * np.repeat(np.exp2(scales.astype(np.float64) - 127.0), 8, axis=1)[..., None]
    return vals.transpose(0, 1, 3, 2).reshape(g * 512, n)


B, N, D, C, H, NS = 4, 2048, 512, 256, 4, 11
HD = C // H
D4 = (0.4829629131445341, 0.8365163037378079, 0.2241438680420134, -0.1294095225512604)


def causal_multiscale(x_c, scale_gain):
    g = np.exp(scale_gain - scale_gain.max(0, keepdims=True))
    gains = g / g.sum(0, keepdims=True)
    gains_exp = np.repeat(gains, HD, axis=1)
    out = np.zeros_like(x_c)
    for j in range(NS):
        d = 2 ** j
        xp = np.pad(x_c, ((0, 0), (0, 0), (3 * d, 0)))
        y = (D4[0] * xp[:, :, 0 * d:0 * d + N]
             + D4[1] * xp[:, :, 1 * d:1 * d + N]
             + D4[2] * xp[:, :, 2 * d:2 * d + N]
             + D4[3] * xp[:, :, 3 * d:3 * d + N])
        out = out + gains_exp[j][None, :, None] * y
    return out


def setup_inputs():
    s = mx_kscale(D)
    x = bf(np.random.standard_normal((B, N, D)) * s)
    k_w = np.random.standard_normal((C, D)) / np.sqrt(D) / s[None, :]
    k_b = bf(np.random.standard_normal(C) * 0.2)
    v_w = np.random.standard_normal((C, D)) / np.sqrt(D) / s[None, :]
    v_b = bf(np.random.standard_normal(C) * 0.2)
    scale_gain = bf(np.random.standard_normal((NS, H)) * 0.5)
    k_w_words, k_w_scales = pack_weight(np.ascontiguousarray(k_w.T), "e4m3")
    v_w_words, v_w_scales = pack_weight(np.ascontiguousarray(v_w.T), "e4m3")
    return {"x": x,
            "k_w_words": k_w_words,
            "k_w_scales": k_w_scales,
            "k_b": k_b,
            "v_w_words": v_w_words,
            "v_w_scales": v_w_scales,
            "v_b": v_b,
            "scale_gain": scale_gain}


def reference(x, k_w_words, k_w_scales, k_b, v_w_words, v_w_scales, v_b, scale_gain):
    xq = mxq(f64(x), 2, "e4m3")
    k = ((xq @ unpack_weight(k_w_words, k_w_scales, "e4m3")) + f64(k_b)).reshape(B, N, H, HD)
    v = ((xq @ unpack_weight(v_w_words, v_w_scales, "e4m3")) + f64(v_b)).reshape(B, N, H, HD)
    k_mag = np.sqrt((k * k).sum(-1, keepdims=True))
    field = v * k_mag
    x_c = field.transpose(0, 2, 3, 1).reshape(B, C, N)
    return causal_multiscale(x_c, f64(scale_gain))

@@ -1,0 +1,290 @@
+from contextlib import ExitStack
+
+import concourse.mybir as mybir
+from concourse.masks import make_identity
+
+F32 = mybir.dt.float32
+BF16 = mybir.dt.bfloat16
+I32 = mybir.dt.int32
+U32 = mybir.dt.uint32
+U8 = mybir.dt.uint8
+FP8X4 = mybir.dt.float8_e4m3fn_x4
+ALU = mybir.AluOpType
+ACT = mybir.ActivationFunctionType
+
+B, N, D, C, H, NS = 4, 2048, 512, 256, 4, 11
+HD = C // H
+TAP0, TAP1, TAP2, TAP3 = 0.4829629131445341, 0.8365163037378079, 0.2241438680420134, -0.1294095225512604
+
+P = 128
+PACK = 4
+BLK = N // P
+TILES = 4
+CHUNK = TILES * P
+CHUNKS = BLK // TILES
+PAIR = 2
+EARLY_A = 32
+EARLY = EARLY_A * BLK
+LATE_A = P - EARLY_A
+PAD = LATE_A - EARLY_A
+
+FLOPS = 2 * B * N * D * 2 * C
+
+
+def tile_causalwaveletfieldattentionbyte_pa_t_kernel(
+    tc, x, k_w_words, k_w_scales, k_b, v_w_words, v_w_scales, v_b, scale_gain, out
+):
+    nc = tc.nc
+    with ExitStack() as stack:
+        const = stack.enter_context(tc.tile_pool(name="const", bufs=1))
+        stage = stack.enter_context(tc.tile_pool(name="stage", bufs=2))
+        work = stack.enter_context(tc.tile_pool(name="work", bufs=2))
+        psum = stack.enter_context(tc.psum_pool(name="psum", bufs=1))
+
+        k_plane = const.tile([P, C], U8, align_bytes=64)
+        v_plane = const.tile([P, C], U8, align_bytes=64)
+        nc.vector.memset(k_plane[:].bitcast(I32), 0)
+        nc.vector.memset(v_plane[:].bitcast(I32), 0)
+        k_words = const.tile([P, C], U32, align_bytes=64)
+        v_words = const.tile([P, C], U32, align_bytes=64)
+
+        def load_x_chunk(index):
+            batch, g = divmod(index, CHUNKS)
+            x_chunk = const.tile([P, TILES, D], BF16, name="x%d" % index)
+            rows = x[batch].rearrange("(a b) k -> a b k", b=BLK)
+            nc.sync.dma_start(out=x_chunk[:], in_=rows[:, g * TILES : (g + 1) * TILES, :])
+            return x_chunk
+
+        def load_weight(words_tile, plane, words, scales):
+            nc.sync.dma_start(
+                out=words_tile[:].bitcast(I32), in_=words[0].rearrange("p n t -> p (n t)").bitcast(I32)
+            )
+            for quadrant in range(4):
+                nc.sync.dma_start(
+                    out=plane[32 * quadrant : 32 * quadrant + 4, :].bitcast(I32),
+                    in_=scales[0, 4 * quadrant : 4 * quadrant + 4, :].bitcast(I32),
+                )
+
+        x_chunks = [load_x_chunk(0)]
+        load_weight(k_words, k_plane, k_w_words, k_w_scales)
+        load_weight(v_words, v_plane, v_w_words, v_w_scales)
+        for index in range(1, B * CHUNKS):
+            x_chunks.append(load_x_chunk(index))
+
+        gain_bf = const.tile([P, NS * H], BF16)
+        nc.scalar.dma_start(out=gain_bf[:], in_=scale_gain.rearrange("j h -> (j h)").partition_broadcast(P))
+        vb_bf = const.tile([P, C], BF16)
+        nc.scalar.dma_start(out=vb_bf[:], in_=v_b.partition_broadcast(P))
+        kb_rows = const.tile([P, P], BF16)
+        nc.vector.memset(kb_rows[:], 0.0)
+        nc.scalar.dma_start(out=kb_rows[0:2, :], in_=k_b.rearrange("(r c) -> r c", r=2))
+
+        shifted = const.tile([P, PAD + P], F32)
+        nc.gpsimd.memset(shifted[:, 0:PAD], 0.0)
+        make_identity(nc, shifted[:, PAD : PAD + P])
+        identity = shifted[:, PAD : PAD + P]
+
+        head_of = const.tile([P, 2, H], F32)
+        nc.vector.memset(head_of[:], 0.0)
+        for half in range(2):
+            for part in range(2):
+                h = 2 * half + part
+                nc.vector.memset(head_of[part * HD : (part + 1) * HD, half, h : h + 1], 1.0)
+
+        kb_f32 = const.tile([P, P], F32)
+        nc.vector.tensor_copy(out=kb_f32[:], in_=kb_rows[:])
+        kb_ps = psum.tile([P, P], F32, tag="f_ps")
+        nc.tensor.transpose(out=kb_ps[:], in_=kb_f32[:], identity=identity)
+        kb_col = const.tile([P, 2], F32)
+        nc.vector.tensor_copy(out=kb_col[:], in_=kb_ps[:, 0:2])
+
+        vb_bc = const.tile([P, H, HD], F32)
+        nc.vector.tensor_copy(out=vb_bc[:], in_=vb_bf[:].rearrange("p (h c) -> p h c", h=H))
+
+        gain = const.tile([P, H, NS], F32)
+        nc.vector.tensor_copy(out=gain[:], in_=gain_bf[:].rearrange("p (j h) -> p h j", h=H))
+        top = const.tile([P, H], F32)
+        nc.vector.tensor_reduce(out=top[:], in_=gain[:], axis=mybir.AxisListType.X, op=ALU.max)
+        nc.vector.tensor_tensor(
+            out=gain[:], in0=gain[:], in1=top[:].unsqueeze(2).to_broadcast([P, H, NS]), op=ALU.subtract
+        )
+        nc.scalar.activation(out=gain[:], in_=gain[:], func=ACT.Exp)
+        total = const.tile([P, H], F32)
+        nc.vector.tensor_reduce(out=total[:], in_=gain[:], axis=mybir.AxisListType.X, op=ALU.add)
+        nc.vector.reciprocal(out=total[:], in_=total[:])
+        nc.vector.tensor_tensor(
+            out=gain[:], in0=gain[:], in1=total[:].unsqueeze(2).to_broadcast([P, H, NS]), op=ALU.mult
+        )
+        coef_pow = const.tile([P, H, NS], F32)
+        nc.vector.tensor_scalar_mul(out=coef_pow[:], in0=gain[:], scalar1=TAP2)
+        nc.vector.scalar_tensor_tensor(
+            out=coef_pow[:, :, 1:NS],
+            in0=gain[:, :, 0 : NS - 1],
+            scalar=TAP1,
+            in1=coef_pow[:, :, 1:NS],
+            op0=ALU.mult,
+            op1=ALU.add,
+        )
+        coef_tri = const.tile([P, H, NS], F32)
+        nc.vector.tensor_scalar_mul(out=coef_tri[:], in0=gain[:], scalar1=TAP0)
+
+        def taps_of(h):
+            taps = [(2**j, coef_pow[:, h, j : j + 1]) for j in range(NS)]
+            taps += [(3 * 2**j, coef_tri[:, h, j : j + 1]) for j in range(NS)]
+            return [tap for tap in taps if tap[0] < N]
+
+        fields = [const.tile([P, BLK, H, PAIR, HD], F32, name="field%d" % pair) for pair in range(B // PAIR)]
+        norms = [const.tile([P, PAIR, BLK, H], F32, name="norm%d" % pair) for pair in range(B // PAIR)]
+
+        def project_chunk(pair, chunk):
+            member, g = divmod(chunk, CHUNKS)
+            x_chunk = x_chunks[pair * PAIR * CHUNKS + chunk]
+
+            grouped = stage.tile([P, CHUNK, PACK], BF16, align_bytes=64)
+            grouped_words = (
+                grouped[:].rearrange("p n t -> p (n t)").bitcast(F32).rearrange("p (i a u) -> p i a u", i=TILES, u=2)
+            )
+            for j in range(TILES // 2):
+                x_ps = psum.tile([P, 2, 2, P], F32, bufs=2)
+                for t in range(2):
+                    words = x_chunk[:, 2 * j + t, :].bitcast(F32)
+                    for u in range(2):
+                        nc.tensor.transpose(out=x_ps[:, t, u, :], in_=words[:, u : D // 2 : 2], identity=identity)
+                nc.scalar.copy(
+                    out=grouped_words[:, 2 * j : 2 * j + 2, :, :], in_=x_ps[:].rearrange("p t u a -> p t a u")
+                )
+            x_codes = stage.tile([P, CHUNK], U32, align_bytes=64, bufs=3)
+            x_plane = stage.tile([P, CHUNK], U8, align_bytes=64, bufs=3)
+            nc.vector.quantize_mx(
+                out=x_codes[:].bitcast(FP8X4), scales=x_plane[:], in_=grouped[:].rearrange("p n t -> p (n t)")
+            )
+
+            squares = []
+            for half in range(2):
+                cols = slice(half * P, (half + 1) * P)
+                k_ps = psum.tile([P, CHUNK], F32, bufs=2)
+                nc.tensor.matmul_mx(
+                    out=k_ps[:],
+                    lhsT=k_words[:, cols].bitcast(FP8X4),
+                    lhsT_scale=k_plane[:, cols],
+                    rhs=x_codes[:].bitcast(FP8X4),
+                    rhs_scale=x_plane[:],
+                    start=True,
+                    stop=True,
+                )
+                square = stage.tile([P, CHUNK], F32, bufs=4)
+                nc.scalar.activation(out=square[:], in_=k_ps[:], func=ACT.Square, bias=kb_col[:, half : half + 1])
+                squares.append(square)
+
+            for j in range(TILES // 2):
+                v_ps = psum.tile([P, 2, H, HD], F32)
+                for t in range(2):
+                    cols = slice((2 * j + t) * P, (2 * j + t + 1) * P)
+                    nc.tensor.matmul_mx(
+                        out=v_ps[:, t, :, :].rearrange("p h c -> p (h c)"),
+                        lhsT=x_codes[:, cols].bitcast(FP8X4),
+                        lhsT_scale=x_plane[:, cols],
+                        rhs=v_words[:].bitcast(FP8X4),
+                        rhs_scale=v_plane[:],
+                        start=True,
+                        stop=True,
+                    )
+                b0 = g * TILES + 2 * j
+                nc.vector.tensor_tensor(
+                    out=fields[pair][:, b0 : b0 + 2, :, member, :],
+                    in0=v_ps[:],
+                    in1=vb_bc[:].unsqueeze(1).to_broadcast([P, 2, H, HD]),
+                    op=ALU.add,
+                )
+
+            m2_ps = psum.tile([P, TILES, H], F32)
+            for i in range(TILES):
+                for half in range(2):
+                    nc.tensor.matmul(
+                        out=m2_ps[:, i, :],
+                        lhsT=squares[half][:, i * P : (i + 1) * P],
+                        rhs=head_of[:, half, :],
+                        start=(half == 0),
+                        stop=(half == 1),
+                    )
+            nc.scalar.activation(
+                out=norms[pair][:, member, g * TILES : (g + 1) * TILES, :], in_=m2_ps[:], func=ACT.Sqrt
+            )
+
+        toeplitz = const.tile([P, H, LATE_A], F32)
+
+        def build_toeplitz(h):
+            nc.vector.tensor_scalar_mul(
+                out=toeplitz[:, h, :], in0=shifted[:, PAD + EARLY_A : PAD + P], scalar1=TAP3
+            )
+            for shift, coef in taps_of(h):
+                if shift % BLK == 0:
+                    first = PAD + EARLY_A - shift // BLK
+                    nc.vector.scalar_tensor_tensor(
+                        out=toeplitz[:, h, :],
+                        in0=shifted[:, first : first + LATE_A],
+                        scalar=coef,
+                        in1=toeplitz[:, h, :],
+                        op0=ALU.mult,
+                        op1=ALU.add,
+                    )
+
+        def add_tap(acc, f_t, shift, coef, first, last):
+            nc.vector.scalar_tensor_tensor(
+                out=acc[:, first:last],
+                in0=f_t[:, first - shift : last - shift],
+                scalar=coef,
+                in1=acc[:, first:last],
+                op0=ALU.mult,
+                op1=ALU.add,
+            )
+
+        def filter_head(pair, h):
+            field = fields[pair]
+            for b in range(BLK):
+                for member in range(PAIR):
+                    nc.scalar.activation(
+                        out=field[:, b, h, member, :],
+                        in_=field[:, b, h, member, :],
+                        func=ACT.Copy,
+                        scale=norms[pair][:, member, b, h : h + 1],
+                    )
+            f_ab = work.tile([P, P, BLK], F32, bufs=2)
+            acc_ab = work.tile([P, P, BLK], F32, bufs=3)
+            for g in range(CHUNKS):
+                f_ps = psum.tile([P, TILES, P], F32)
+                late_ps = psum.tile([P, TILES, LATE_A], F32)
+                for i in range(TILES):
+                    block = field[:, g * TILES + i, h, :, :].rearrange("p m c -> p (m c)")
+                    nc.tensor.transpose(out=f_ps[:, i, :], in_=block, identity=identity)
+                    nc.tensor.matmul(out=late_ps[:, i, :], lhsT=block, rhs=toeplitz[:, h, :], start=True, stop=True)
+                cols = slice(g * TILES, (g + 1) * TILES)
+                nc.scalar.copy(out=f_ab[:, :, cols], in_=f_ps[:].rearrange("p i a -> p a i"))
+                nc.scalar.copy(out=acc_ab[:, EARLY_A:P, cols], in_=late_ps[:].rearrange("p i a -> p a i"))
+            f_t = f_ab[:].rearrange("p a b -> p (a b)")
+            acc = acc_ab[:].rearrange("p a b -> p (a b)")
+            nc.scalar.mul(out=acc[:, 0:EARLY], in_=f_t[:, 0:EARLY], mul=TAP3)
+
+            taps = taps_of(h)
+            for shift, coef in taps:
+                if shift % BLK != 0:
+                    add_tap(acc, f_t, shift, coef, EARLY, N)
+            for shift, coef in taps:
+                if shift < EARLY:
+                    add_tap(acc, f_t, shift, coef, shift, EARLY)
+            for member in range(PAIR):
+                nc.sync.dma_start(
+                    out=out[pair * PAIR + member, h * HD : (h + 1) * HD, :],
+                    in_=acc[member * HD : (member + 1) * HD, :],
+                )
+
+        for chunk in range(PAIR * CHUNKS):
+            project_chunk(0, chunk)
+        for h in range(H):
+            build_toeplitz(h)
+        for pair in range(B // PAIR):
+            for h in range(H):
+                filter_head(pair, h)
+                if pair + 1 < B // PAIR:
+                    for chunk in range(2 * h, 2 * h + 2):
+                        project_chunk(pair + 1, chunk)

@@ -27,6 +27,7 @@ EARLY_A = 32
 EARLY = EARLY_A * BLK
 LATE_A = P - EARLY_A
 PAD = LATE_A - EARLY_A
+LATE_HALF = (N - EARLY) // 2
 
 FLOPS = 2 * B * N * D * 2 * C
 
@@ -84,12 +85,10 @@ def tile_causalwaveletfieldattentionbyte_pa_t_kernel(
         make_identity(nc, shifted[:, PAD : PAD + P])
         identity = shifted[:, PAD : PAD + P]
 
-        head_of = const.tile([P, 2, H], F32)
+        head_of = const.tile([P, 2], F32)
         nc.vector.memset(head_of[:], 0.0)
-        for half in range(2):
-            for part in range(2):
-                h = 2 * half + part
-                nc.vector.memset(head_of[part * HD : (part + 1) * HD, half, h : h + 1], 1.0)
+        for part in range(2):
+            nc.vector.memset(head_of[part * HD : (part + 1) * HD, part : part + 1], 1.0)
 
         kb_f32 = const.tile([P, P], F32)
         nc.vector.tensor_copy(out=kb_f32[:], in_=kb_rows[:])
@@ -136,6 +135,8 @@ def tile_causalwaveletfieldattentionbyte_pa_t_kernel(
         fields = [const.tile([P, BLK, H, PAIR, HD], F32, name="field%d" % pair) for pair in range(B // PAIR)]
         norms = [const.tile([P, PAIR, BLK, H], F32, name="norm%d" % pair) for pair in range(B // PAIR)]
 
+        quantised = {}
+
         def project_chunk(pair, chunk):
             member, g = divmod(chunk, CHUNKS)
             x_chunk = x_chunks[pair * PAIR * CHUNKS + chunk]
@@ -153,28 +154,12 @@ def tile_causalwaveletfieldattentionbyte_pa_t_kernel(
                 nc.scalar.copy(
                     out=grouped_words[:, 2 * j : 2 * j + 2, :, :], in_=x_ps[:].rearrange("p t u a -> p t a u")
                 )
-            x_codes = stage.tile([P, CHUNK], U32, align_bytes=64, bufs=3)
-            x_plane = stage.tile([P, CHUNK], U8, align_bytes=64, bufs=3)
+            x_codes = stage.tile([P, CHUNK], U32, align_bytes=64, bufs=PAIR * CHUNKS)
+            x_plane = stage.tile([P, CHUNK], U8, align_bytes=64, bufs=PAIR * CHUNKS)
+            quantised[(pair, chunk)] = (x_codes, x_plane)
             nc.vector.quantize_mx(
                 out=x_codes[:].bitcast(FP8X4), scales=x_plane[:], in_=grouped[:].rearrange("p n t -> p (n t)")
             )
-
-            squares = []
-            for half in range(2):
-                cols = slice(half * P, (half + 1) * P)
-                k_ps = psum.tile([P, CHUNK], F32, bufs=2)
-                nc.tensor.matmul_mx(
-                    out=k_ps[:],
-                    lhsT=k_words[:, cols].bitcast(FP8X4),
-                    lhsT_scale=k_plane[:, cols],
-                    rhs=x_codes[:].bitcast(FP8X4),
-                    rhs_scale=x_plane[:],
-                    start=True,
-                    stop=True,
-                )
-                square = stage.tile([P, CHUNK], F32, bufs=4)
-                nc.scalar.activation(out=square[:], in_=k_ps[:], func=ACT.Square, bias=kb_col[:, half : half + 1])
-                squares.append(square)
 
             for j in range(TILES // 2):
                 v_ps = psum.tile([P, 2, H, HD], F32)
@@ -197,37 +182,53 @@ def tile_causalwaveletfieldattentionbyte_pa_t_kernel(
                     op=ALU.add,
                 )
 
-            m2_ps = psum.tile([P, TILES, H], F32)
+        def norm_chunk(pair, chunk, half):
+            member, g = divmod(chunk, CHUNKS)
+            x_codes, x_plane = quantised[(pair, chunk)]
+            cols = slice(half * P, (half + 1) * P)
+            k_ps = psum.tile([P, CHUNK], F32, bufs=2)
+            nc.tensor.matmul_mx(
+                out=k_ps[:],
+                lhsT=k_words[:, cols].bitcast(FP8X4),
+                lhsT_scale=k_plane[:, cols],
+                rhs=x_codes[:].bitcast(FP8X4),
+                rhs_scale=x_plane[:],
+                start=True,
+                stop=True,
+            )
+            square = stage.tile([P, CHUNK], F32, bufs=3)
+            nc.scalar.activation(out=square[:], in_=k_ps[:], func=ACT.Square, bias=kb_col[:, half : half + 1])
+            m2_ps = psum.tile([P, TILES, 2], F32)
             for i in range(TILES):
-                for half in range(2):
-                    nc.tensor.matmul(
-                        out=m2_ps[:, i, :],
-                        lhsT=squares[half][:, i * P : (i + 1) * P],
-                        rhs=head_of[:, half, :],
-                        start=(half == 0),
-                        stop=(half == 1),
-                    )
+                nc.tensor.matmul(
+                    out=m2_ps[:, i, :], lhsT=square[:, i * P : (i + 1) * P], rhs=head_of[:], start=True, stop=True
+                )
             nc.scalar.activation(
-                out=norms[pair][:, member, g * TILES : (g + 1) * TILES, :], in_=m2_ps[:], func=ACT.Sqrt
+                out=norms[pair][:, member, g * TILES : (g + 1) * TILES, 2 * half : 2 * half + 2],
+                in_=m2_ps[:],
+                func=ACT.Sqrt,
             )
 
         toeplitz = const.tile([P, H, LATE_A], F32)
 
-        def build_toeplitz(h):
-            nc.vector.tensor_scalar_mul(
-                out=toeplitz[:, h, :], in0=shifted[:, PAD + EARLY_A : PAD + P], scalar1=TAP3
-            )
-            for shift, coef in taps_of(h):
-                if shift % BLK == 0:
-                    first = PAD + EARLY_A - shift // BLK
-                    nc.vector.scalar_tensor_tensor(
-                        out=toeplitz[:, h, :],
-                        in0=shifted[:, first : first + LATE_A],
-                        scalar=coef,
-                        in1=toeplitz[:, h, :],
-                        op0=ALU.mult,
-                        op1=ALU.add,
-                    )
+        def build_toeplitz():
+            for h in range(H):
+                nc.vector.tensor_scalar_mul(
+                    out=toeplitz[:, h, :], in0=shifted[:, PAD + EARLY_A : PAD + P], scalar1=TAP3
+                )
+            for index in range(len(taps_of(0))):
+                for h in range(H):
+                    shift, coef = taps_of(h)[index]
+                    if shift % BLK == 0:
+                        first = PAD + EARLY_A - shift // BLK
+                        nc.vector.scalar_tensor_tensor(
+                            out=toeplitz[:, h, :],
+                            in0=shifted[:, first : first + LATE_A],
+                            scalar=coef,
+                            in1=toeplitz[:, h, :],
+                            op0=ALU.mult,
+                            op1=ALU.add,
+                        )
 
         def add_tap(acc, f_t, shift, coef, first, last):
             nc.vector.scalar_tensor_tensor(
@@ -266,25 +267,37 @@ def tile_causalwaveletfieldattentionbyte_pa_t_kernel(
             nc.scalar.mul(out=acc[:, 0:EARLY], in_=f_t[:, 0:EARLY], mul=TAP3)
 
             taps = taps_of(h)
-            for shift, coef in taps:
-                if shift % BLK != 0:
-                    add_tap(acc, f_t, shift, coef, EARLY, N)
-            for shift, coef in taps:
-                if shift < EARLY:
-                    add_tap(acc, f_t, shift, coef, shift, EARLY)
+            early = [tap for tap in taps if tap[0] < EARLY]
+            late = [(tap, first) for tap in taps if tap[0] % BLK != 0 for first in (EARLY, EARLY + LATE_HALF)]
+            for k in range(len(early)):
+                shift, coef = early[k]
+                add_tap(acc, f_t, shift, coef, shift, EARLY)
+                if k < len(late):
+                    (shift, coef), first = late[k]
+                    add_tap(acc, f_t, shift, coef, first, first + LATE_HALF)
             for member in range(PAIR):
                 nc.sync.dma_start(
                     out=out[pair * PAIR + member, h * HD : (h + 1) * HD, :],
                     in_=acc[member * HD : (member + 1) * HD, :],
                 )
 
-        for chunk in range(PAIR * CHUNKS):
-            project_chunk(0, chunk)
-        for h in range(H):
-            build_toeplitz(h)
+        def prepare(pair, chunks):
+            for chunk in chunks:
+                project_chunk(pair, chunk)
+                norm_chunk(pair, chunk, 0)
+
+        chunks = PAIR * CHUNKS
+        prepare(0, range(chunks))
+        build_toeplitz()
         for pair in range(B // PAIR):
-            for h in range(H):
-                filter_head(pair, h)
-                if pair + 1 < B // PAIR:
-                    for chunk in range(2 * h, 2 * h + 2):
-                        project_chunk(pair + 1, chunk)
+            more = pair + 1 < B // PAIR
+            filter_head(pair, 0)
+            for chunk in range(chunks):
+                norm_chunk(pair, chunk, 1)
+            filter_head(pair, 1)
+            if more:
+                prepare(pair + 1, range(0, chunks // 2))
+            filter_head(pair, 2)
+            if more:
+                prepare(pair + 1, range(chunks // 2, chunks))
+            filter_head(pair, 3)

@@ -23,11 +23,11 @@ TILES = 4
 CHUNK = TILES * P
 CHUNKS = BLK // TILES
 PAIR = 2
-EARLY_A = 32
+EARLY_A = 28
 EARLY = EARLY_A * BLK
 LATE_A = P - EARLY_A
-PAD = LATE_A - EARLY_A
-LATE_HALF = (N - EARLY) // 2
+MAX_SHIFT_A = 3 * 2 ** (NS - 2) // BLK
+PAD = MAX_SHIFT_A - EARLY_A
 
 FLOPS = 2 * B * N * D * 2 * C
 
@@ -49,12 +49,14 @@ def tile_causalwaveletfieldattentionbyte_pa_t_kernel(
         k_words = const.tile([P, C], U32, align_bytes=64)
         v_words = const.tile([P, C], U32, align_bytes=64)
 
-        def load_x_chunk(index):
-            batch, g = divmod(index, CHUNKS)
-            x_chunk = const.tile([P, TILES, D], BF16, name="x%d" % index)
-            rows = x[batch].rearrange("(a b) k -> a b k", b=BLK)
+        x_chunks = {}
+
+        def load_x_chunk(pair, chunk):
+            g, member = divmod(chunk, PAIR)
+            x_chunk = stage.tile([P, TILES, D], BF16, bufs=PAIR * CHUNKS)
+            rows = x[pair * PAIR + member].rearrange("(a b) k -> a b k", b=BLK)
             nc.sync.dma_start(out=x_chunk[:], in_=rows[:, g * TILES : (g + 1) * TILES, :])
-            return x_chunk
+            x_chunks[(pair, chunk)] = x_chunk
 
         def load_weight(words_tile, plane, words, scales):
             nc.sync.dma_start(
@@ -66,11 +68,11 @@ def tile_causalwaveletfieldattentionbyte_pa_t_kernel(
                     in_=scales[0, 4 * quadrant : 4 * quadrant + 4, :].bitcast(I32),
                 )
 
-        x_chunks = [load_x_chunk(0)]
+        load_x_chunk(0, 0)
         load_weight(k_words, k_plane, k_w_words, k_w_scales)
         load_weight(v_words, v_plane, v_w_words, v_w_scales)
-        for index in range(1, B * CHUNKS):
-            x_chunks.append(load_x_chunk(index))
+        for chunk in range(1, PAIR * CHUNKS):
+            load_x_chunk(0, chunk)
 
         gain_bf = const.tile([P, NS * H], BF16)
         nc.scalar.dma_start(out=gain_bf[:], in_=scale_gain.rearrange("j h -> (j h)").partition_broadcast(P))
@@ -92,7 +94,7 @@ def tile_causalwaveletfieldattentionbyte_pa_t_kernel(
 
         kb_f32 = const.tile([P, P], F32)
         nc.vector.tensor_copy(out=kb_f32[:], in_=kb_rows[:])
-        kb_ps = psum.tile([P, P], F32, tag="f_ps")
+        kb_ps = psum.tile([P, P], F32, tag="turned", bufs=3)
         nc.tensor.transpose(out=kb_ps[:], in_=kb_f32[:], identity=identity)
         kb_col = const.tile([P, 2], F32)
         nc.vector.tensor_copy(out=kb_col[:], in_=kb_ps[:, 0:2])
@@ -138,22 +140,21 @@ def tile_causalwaveletfieldattentionbyte_pa_t_kernel(
         quantised = {}
 
         def project_chunk(pair, chunk):
-            member, g = divmod(chunk, CHUNKS)
-            x_chunk = x_chunks[pair * PAIR * CHUNKS + chunk]
+            g, member = divmod(chunk, PAIR)
+            x_chunk = x_chunks[(pair, chunk)]
+            copy_out = nc.vector.tensor_copy if pair == 0 else nc.scalar.copy
 
             grouped = stage.tile([P, CHUNK, PACK], BF16, align_bytes=64)
             grouped_words = (
                 grouped[:].rearrange("p n t -> p (n t)").bitcast(F32).rearrange("p (i a u) -> p i a u", i=TILES, u=2)
             )
             for j in range(TILES // 2):
-                x_ps = psum.tile([P, 2, 2, P], F32, bufs=2)
+                x_ps = psum.tile([P, 2, 2, P], F32, tag="turned", bufs=3)
                 for t in range(2):
                     words = x_chunk[:, 2 * j + t, :].bitcast(F32)
                     for u in range(2):
                         nc.tensor.transpose(out=x_ps[:, t, u, :], in_=words[:, u : D // 2 : 2], identity=identity)
-                nc.scalar.copy(
-                    out=grouped_words[:, 2 * j : 2 * j + 2, :, :], in_=x_ps[:].rearrange("p t u a -> p t a u")
-                )
+                copy_out(out=grouped_words[:, 2 * j : 2 * j + 2, :, :], in_=x_ps[:].rearrange("p t u a -> p t a u"))
             x_codes = stage.tile([P, CHUNK], U32, align_bytes=64, bufs=PAIR * CHUNKS)
             x_plane = stage.tile([P, CHUNK], U8, align_bytes=64, bufs=PAIR * CHUNKS)
             quantised[(pair, chunk)] = (x_codes, x_plane)
@@ -162,7 +163,7 @@ def tile_causalwaveletfieldattentionbyte_pa_t_kernel(
             )
 
             for j in range(TILES // 2):
-                v_ps = psum.tile([P, 2, H, HD], F32)
+                v_ps = psum.tile([P, 2, H, HD], F32, bufs=2)
                 for t in range(2):
                     cols = slice((2 * j + t) * P, (2 * j + t + 1) * P)
                     nc.tensor.matmul_mx(
@@ -183,10 +184,10 @@ def tile_causalwaveletfieldattentionbyte_pa_t_kernel(
                 )
 
         def norm_chunk(pair, chunk, half):
-            member, g = divmod(chunk, CHUNKS)
+            g, member = divmod(chunk, PAIR)
             x_codes, x_plane = quantised[(pair, chunk)]
             cols = slice(half * P, (half + 1) * P)
-            k_ps = psum.tile([P, CHUNK], F32, bufs=2)
+            k_ps = psum.tile([P, CHUNK], F32)
             nc.tensor.matmul_mx(
                 out=k_ps[:],
                 lhsT=k_words[:, cols].bitcast(FP8X4),
@@ -198,7 +199,7 @@ def tile_causalwaveletfieldattentionbyte_pa_t_kernel(
             )
             square = stage.tile([P, CHUNK], F32, bufs=3)
             nc.scalar.activation(out=square[:], in_=k_ps[:], func=ACT.Square, bias=kb_col[:, half : half + 1])
-            m2_ps = psum.tile([P, TILES, 2], F32)
+            m2_ps = psum.tile([P, TILES, 2], F32, tag="sums", bufs=2)
             for i in range(TILES):
                 nc.tensor.matmul(
                     out=m2_ps[:, i, :], lhsT=square[:, i * P : (i + 1) * P], rhs=head_of[:], start=True, stop=True
@@ -240,21 +241,21 @@ def tile_causalwaveletfieldattentionbyte_pa_t_kernel(
                 op1=ALU.add,
             )
 
-        def filter_head(pair, h):
+        def turn_head(pair, h):
             field = fields[pair]
-            for b in range(BLK):
-                for member in range(PAIR):
-                    nc.scalar.activation(
-                        out=field[:, b, h, member, :],
-                        in_=field[:, b, h, member, :],
-                        func=ACT.Copy,
-                        scale=norms[pair][:, member, b, h : h + 1],
-                    )
-            f_ab = work.tile([P, P, BLK], F32, bufs=2)
-            acc_ab = work.tile([P, P, BLK], F32, bufs=3)
+            f_ab = work.tile([P, P, BLK], F32, bufs=4)
+            acc_ab = work.tile([P, P, BLK], F32, bufs=4)
             for g in range(CHUNKS):
-                f_ps = psum.tile([P, TILES, P], F32)
-                late_ps = psum.tile([P, TILES, LATE_A], F32)
+                for b in range(g * TILES, (g + 1) * TILES):
+                    for member in range(PAIR):
+                        nc.scalar.activation(
+                            out=field[:, b, h, member, :],
+                            in_=field[:, b, h, member, :],
+                            func=ACT.Copy,
+                            scale=norms[pair][:, member, b, h : h + 1],
+                        )
+                f_ps = psum.tile([P, TILES, P], F32, tag="turned", bufs=3)
+                late_ps = psum.tile([P, TILES, LATE_A], F32, tag="sums", bufs=2)
                 for i in range(TILES):
                     block = field[:, g * TILES + i, h, :, :].rearrange("p m c -> p (m c)")
                     nc.tensor.transpose(out=f_ps[:, i, :], in_=block, identity=identity)
@@ -266,38 +267,37 @@ def tile_causalwaveletfieldattentionbyte_pa_t_kernel(
             acc = acc_ab[:].rearrange("p a b -> p (a b)")
             nc.scalar.mul(out=acc[:, 0:EARLY], in_=f_t[:, 0:EARLY], mul=TAP3)
 
-            taps = taps_of(h)
-            early = [tap for tap in taps if tap[0] < EARLY]
-            late = [(tap, first) for tap in taps if tap[0] % BLK != 0 for first in (EARLY, EARLY + LATE_HALF)]
-            for k in range(len(early)):
-                shift, coef = early[k]
-                add_tap(acc, f_t, shift, coef, shift, EARLY)
-                if k < len(late):
-                    (shift, coef), first = late[k]
-                    add_tap(acc, f_t, shift, coef, first, first + LATE_HALF)
-            for member in range(PAIR):
-                nc.sync.dma_start(
-                    out=out[pair * PAIR + member, h * HD : (h + 1) * HD, :],
-                    in_=acc[member * HD : (member + 1) * HD, :],
-                )
+            return f_t, acc
 
-        def prepare(pair, chunks):
-            for chunk in chunks:
+        def filter_heads(pair, half):
+            heads = (2 * half, 2 * half + 1)
+            turned = [turn_head(pair, h) for h in heads]
+            for index in range(len(taps_of(0))):
+                for h, (f_t, acc) in zip(heads, turned):
+                    shift, coef = taps_of(h)[index]
+                    last = EARLY if shift % BLK == 0 else N
+                    if shift < last:
+                        add_tap(acc, f_t, shift, coef, shift, last)
+            for h, (f_t, acc) in zip(heads, turned):
+                for member in range(PAIR):
+                    nc.sync.dma_start(
+                        out=out[pair * PAIR + member, h * HD : (h + 1) * HD, :],
+                        in_=acc[member * HD : (member + 1) * HD, :],
+                    )
+
+        def prepare(pair):
+            for chunk in range(PAIR * CHUNKS):
                 project_chunk(pair, chunk)
                 norm_chunk(pair, chunk, 0)
 
-        chunks = PAIR * CHUNKS
-        prepare(0, range(chunks))
+        prepare(0)
         build_toeplitz()
         for pair in range(B // PAIR):
-            more = pair + 1 < B // PAIR
-            filter_head(pair, 0)
-            for chunk in range(chunks):
+            filter_heads(pair, 0)
+            for chunk in range(PAIR * CHUNKS):
                 norm_chunk(pair, chunk, 1)
-            filter_head(pair, 1)
-            if more:
-                prepare(pair + 1, range(0, chunks // 2))
-            filter_head(pair, 2)
-            if more:
-                prepare(pair + 1, range(chunks // 2, chunks))
-            filter_head(pair, 3)
+            if pair + 1 < B // PAIR:
+                for chunk in range(PAIR * CHUNKS):
+                    load_x_chunk(pair + 1, chunk)
+                prepare(pair + 1)
+            filter_heads(pair, 1)

@@ -28,6 +28,7 @@ EARLY = EARLY_A * BLK
 LATE_A = P - EARLY_A
 MAX_SHIFT_A = 3 * 2 ** (NS - 2) // BLK
 PAD = MAX_SHIFT_A - EARLY_A
+LATE_HALF = (N - EARLY) // 2
 
 FLOPS = 2 * B * N * D * 2 * C
 
@@ -49,14 +50,12 @@ def tile_causalwaveletfieldattentionbyte_pa_t_kernel(
         k_words = const.tile([P, C], U32, align_bytes=64)
         v_words = const.tile([P, C], U32, align_bytes=64)
 
-        x_chunks = {}
-
-        def load_x_chunk(pair, chunk):
-            g, member = divmod(chunk, PAIR)
-            x_chunk = stage.tile([P, TILES, D], BF16, bufs=PAIR * CHUNKS)
-            rows = x[pair * PAIR + member].rearrange("(a b) k -> a b k", b=BLK)
+        def load_x_chunk(index):
+            batch, g = divmod(index, CHUNKS)
+            x_chunk = const.tile([P, TILES, D], BF16, name="x%d" % index)
+            rows = x[batch].rearrange("(a b) k -> a b k", b=BLK)
             nc.sync.dma_start(out=x_chunk[:], in_=rows[:, g * TILES : (g + 1) * TILES, :])
-            x_chunks[(pair, chunk)] = x_chunk
+            return x_chunk
 
         def load_weight(words_tile, plane, words, scales):
             nc.sync.dma_start(
@@ -68,11 +67,11 @@ def tile_causalwaveletfieldattentionbyte_pa_t_kernel(
                     in_=scales[0, 4 * quadrant : 4 * quadrant + 4, :].bitcast(I32),
                 )
 
-        load_x_chunk(0, 0)
+        x_chunks = [load_x_chunk(0)]
         load_weight(k_words, k_plane, k_w_words, k_w_scales)
         load_weight(v_words, v_plane, v_w_words, v_w_scales)
-        for chunk in range(1, PAIR * CHUNKS):
-            load_x_chunk(0, chunk)
+        for index in range(1, B * CHUNKS):
+            x_chunks.append(load_x_chunk(index))
 
         gain_bf = const.tile([P, NS * H], BF16)
         nc.scalar.dma_start(out=gain_bf[:], in_=scale_gain.rearrange("j h -> (j h)").partition_broadcast(P))
@@ -94,7 +93,7 @@ def tile_causalwaveletfieldattentionbyte_pa_t_kernel(
 
         kb_f32 = const.tile([P, P], F32)
         nc.vector.tensor_copy(out=kb_f32[:], in_=kb_rows[:])
-        kb_ps = psum.tile([P, P], F32, tag="turned", bufs=3)
+        kb_ps = psum.tile([P, P], F32, tag="f_ps")
         nc.tensor.transpose(out=kb_ps[:], in_=kb_f32[:], identity=identity)
         kb_col = const.tile([P, 2], F32)
         nc.vector.tensor_copy(out=kb_col[:], in_=kb_ps[:, 0:2])
@@ -139,22 +138,22 @@ def tile_causalwaveletfieldattentionbyte_pa_t_kernel(
 
         quantised = {}
 
-        def project_chunk(pair, chunk):
-            g, member = divmod(chunk, PAIR)
-            x_chunk = x_chunks[(pair, chunk)]
-            copy_out = nc.vector.tensor_copy if pair == 0 else nc.scalar.copy
+        def quantise_chunk(pair, chunk):
+            x_chunk = x_chunks[pair * PAIR * CHUNKS + chunk]
 
             grouped = stage.tile([P, CHUNK, PACK], BF16, align_bytes=64)
             grouped_words = (
                 grouped[:].rearrange("p n t -> p (n t)").bitcast(F32).rearrange("p (i a u) -> p i a u", i=TILES, u=2)
             )
             for j in range(TILES // 2):
-                x_ps = psum.tile([P, 2, 2, P], F32, tag="turned", bufs=3)
+                x_ps = psum.tile([P, 2, 2, P], F32, bufs=2)
                 for t in range(2):
                     words = x_chunk[:, 2 * j + t, :].bitcast(F32)
                     for u in range(2):
                         nc.tensor.transpose(out=x_ps[:, t, u, :], in_=words[:, u : D // 2 : 2], identity=identity)
-                copy_out(out=grouped_words[:, 2 * j : 2 * j + 2, :, :], in_=x_ps[:].rearrange("p t u a -> p t a u"))
+                nc.scalar.copy(
+                    out=grouped_words[:, 2 * j : 2 * j + 2, :, :], in_=x_ps[:].rearrange("p t u a -> p t a u")
+                )
             x_codes = stage.tile([P, CHUNK], U32, align_bytes=64, bufs=PAIR * CHUNKS)
             x_plane = stage.tile([P, CHUNK], U8, align_bytes=64, bufs=PAIR * CHUNKS)
             quantised[(pair, chunk)] = (x_codes, x_plane)
@@ -162,8 +161,11 @@ def tile_causalwaveletfieldattentionbyte_pa_t_kernel(
                 out=x_codes[:].bitcast(FP8X4), scales=x_plane[:], in_=grouped[:].rearrange("p n t -> p (n t)")
             )
 
+        def value_chunk(pair, chunk):
+            member, g = divmod(chunk, CHUNKS)
+            x_codes, x_plane = quantised[(pair, chunk)]
             for j in range(TILES // 2):
-                v_ps = psum.tile([P, 2, H, HD], F32, bufs=2)
+                v_ps = psum.tile([P, 2, H, HD], F32)
                 for t in range(2):
                     cols = slice((2 * j + t) * P, (2 * j + t + 1) * P)
                     nc.tensor.matmul_mx(
@@ -184,10 +186,10 @@ def tile_causalwaveletfieldattentionbyte_pa_t_kernel(
                 )
 
         def norm_chunk(pair, chunk, half):
-            g, member = divmod(chunk, PAIR)
+            member, g = divmod(chunk, CHUNKS)
             x_codes, x_plane = quantised[(pair, chunk)]
             cols = slice(half * P, (half + 1) * P)
-            k_ps = psum.tile([P, CHUNK], F32)
+            k_ps = psum.tile([P, CHUNK], F32, bufs=2)
             nc.tensor.matmul_mx(
                 out=k_ps[:],
                 lhsT=k_words[:, cols].bitcast(FP8X4),
@@ -199,7 +201,7 @@ def tile_causalwaveletfieldattentionbyte_pa_t_kernel(
             )
             square = stage.tile([P, CHUNK], F32, bufs=3)
             nc.scalar.activation(out=square[:], in_=k_ps[:], func=ACT.Square, bias=kb_col[:, half : half + 1])
-            m2_ps = psum.tile([P, TILES, 2], F32, tag="sums", bufs=2)
+            m2_ps = psum.tile([P, TILES, 2], F32)
             for i in range(TILES):
                 nc.tensor.matmul(
                     out=m2_ps[:, i, :], lhsT=square[:, i * P : (i + 1) * P], rhs=head_of[:], start=True, stop=True
@@ -241,21 +243,21 @@ def tile_causalwaveletfieldattentionbyte_pa_t_kernel(
                 op1=ALU.add,
             )
 
-        def turn_head(pair, h):
+        def filter_head(pair, h):
             field = fields[pair]
-            f_ab = work.tile([P, P, BLK], F32, bufs=4)
-            acc_ab = work.tile([P, P, BLK], F32, bufs=4)
+            for b in range(BLK):
+                for member in range(PAIR):
+                    nc.scalar.activation(
+                        out=field[:, b, h, member, :],
+                        in_=field[:, b, h, member, :],
+                        func=ACT.Copy,
+                        scale=norms[pair][:, member, b, h : h + 1],
+                    )
+            f_ab = work.tile([P, P, BLK], F32, bufs=2)
+            acc_ab = work.tile([P, P, BLK], F32, bufs=3)
             for g in range(CHUNKS):
-                for b in range(g * TILES, (g + 1) * TILES):
-                    for member in range(PAIR):
-                        nc.scalar.activation(
-                            out=field[:, b, h, member, :],
-                            in_=field[:, b, h, member, :],
-                            func=ACT.Copy,
-                            scale=norms[pair][:, member, b, h : h + 1],
-                        )
-                f_ps = psum.tile([P, TILES, P], F32, tag="turned", bufs=3)
-                late_ps = psum.tile([P, TILES, LATE_A], F32, tag="sums", bufs=2)
+                f_ps = psum.tile([P, TILES, P], F32)
+                late_ps = psum.tile([P, TILES, LATE_A], F32)
                 for i in range(TILES):
                     block = field[:, g * TILES + i, h, :, :].rearrange("p m c -> p (m c)")
                     nc.tensor.transpose(out=f_ps[:, i, :], in_=block, identity=identity)
@@ -267,37 +269,42 @@ def tile_causalwaveletfieldattentionbyte_pa_t_kernel(
             acc = acc_ab[:].rearrange("p a b -> p (a b)")
             nc.scalar.mul(out=acc[:, 0:EARLY], in_=f_t[:, 0:EARLY], mul=TAP3)
 
-            return f_t, acc
-
-        def filter_heads(pair, half):
-            heads = (2 * half, 2 * half + 1)
-            turned = [turn_head(pair, h) for h in heads]
-            for index in range(len(taps_of(0))):
-                for h, (f_t, acc) in zip(heads, turned):
-                    shift, coef = taps_of(h)[index]
-                    last = EARLY if shift % BLK == 0 else N
-                    if shift < last:
-                        add_tap(acc, f_t, shift, coef, shift, last)
-            for h, (f_t, acc) in zip(heads, turned):
+            taps = taps_of(h)
+            early = [tap for tap in taps if tap[0] < EARLY]
+            late = [(tap, first) for tap in taps if tap[0] % BLK != 0 for first in (EARLY, EARLY + LATE_HALF)]
+            for k in range(len(early)):
+                shift, coef = early[k]
+                add_tap(acc, f_t, shift, coef, shift, EARLY)
+                if k < len(late):
+                    (shift, coef), first = late[k]
+                    add_tap(acc, f_t, shift, coef, first, first + LATE_HALF)
+            for first, last in ((EARLY, EARLY + LATE_HALF), (EARLY + LATE_HALF, N), (0, EARLY)):
                 for member in range(PAIR):
                     nc.sync.dma_start(
-                        out=out[pair * PAIR + member, h * HD : (h + 1) * HD, :],
-                        in_=acc[member * HD : (member + 1) * HD, :],
+                        out=out[pair * PAIR + member, h * HD : (h + 1) * HD, first:last],
+                        in_=acc[member * HD : (member + 1) * HD, first:last],
                     )
 
-        def prepare(pair):
-            for chunk in range(PAIR * CHUNKS):
-                project_chunk(pair, chunk)
-                norm_chunk(pair, chunk, 0)
+        def prepare(pair, chunks):
+            for step in range(len(chunks) + 1):
+                if step < len(chunks):
+                    quantise_chunk(pair, chunks[step])
+                if step > 0:
+                    value_chunk(pair, chunks[step - 1])
+                    norm_chunk(pair, chunks[step - 1], 0)
 
-        prepare(0)
+        chunks = PAIR * CHUNKS
+        prepare(0, range(chunks))
         build_toeplitz()
         for pair in range(B // PAIR):
-            filter_heads(pair, 0)
-            for chunk in range(PAIR * CHUNKS):
+            more = pair + 1 < B // PAIR
+            filter_head(pair, 0)
+            for chunk in range(chunks):
                 norm_chunk(pair, chunk, 1)
-            if pair + 1 < B // PAIR:
-                for chunk in range(PAIR * CHUNKS):
-                    load_x_chunk(pair + 1, chunk)
-                prepare(pair + 1)
-            filter_heads(pair, 1)
+            filter_head(pair, 1)
+            if more:
+                prepare(pair + 1, range(0, chunks // 2))
+            filter_head(pair, 2)
+            if more:
+                prepare(pair + 1, range(chunks // 2, chunks))
+            filter_head(pair, 3)

@@ -29,6 +29,8 @@ LATE_A = P - EARLY_A
 MAX_SHIFT_A = 3 * 2 ** (NS - 2) // BLK
 PAD = MAX_SHIFT_A - EARLY_A
 LATE_HALF = (N - EARLY) // 2
+PERIOD = LATE_A + P - 1
+PITCH = 104
 
 FLOPS = 2 * B * N * D * 2 * C
 
@@ -67,11 +69,12 @@ def tile_causalwaveletfieldattentionbyte_pa_t_kernel(
                     in_=scales[0, 4 * quadrant : 4 * quadrant + 4, :].bitcast(I32),
                 )
 
-        x_chunks = [load_x_chunk(0)]
+        by_turns = [member * CHUNKS + g for g in range(CHUNKS) for member in range(PAIR)]
+        x_chunks = {by_turns[0]: load_x_chunk(by_turns[0])}
         load_weight(k_words, k_plane, k_w_words, k_w_scales)
         load_weight(v_words, v_plane, v_w_words, v_w_scales)
-        for index in range(1, B * CHUNKS):
-            x_chunks.append(load_x_chunk(index))
+        for index in by_turns[1:]:
+            x_chunks[index] = load_x_chunk(index)
 
         gain_bf = const.tile([P, NS * H], BF16)
         nc.scalar.dma_start(out=gain_bf[:], in_=scale_gain.rearrange("j h -> (j h)").partition_broadcast(P))
@@ -212,26 +215,32 @@ def tile_causalwaveletfieldattentionbyte_pa_t_kernel(
                 func=ACT.Sqrt,
             )
 
-        toeplitz = const.tile([P, H, LATE_A], F32)
+        toeplitz = const.tile([P, H, PITCH], F32)
 
         def build_toeplitz():
+            diagonal = const.tile([P, H, PERIOD], F32)
+            nc.gpsimd.memset(diagonal[:], 0.0)
+            place = (0 - EARLY_A) % PERIOD
+            nc.gpsimd.tensor_scalar(
+                out=diagonal[:, :, place : place + 1],
+                in0=coef_pow[:, :, 0:1],
+                scalar1=0.0,
+                scalar2=TAP3,
+                op0=ALU.mult,
+                op1=ALU.add,
+            )
+            for j in range(NS):
+                for shift, coefs in ((2**j, coef_pow), (3 * 2**j, coef_tri)):
+                    if shift % BLK == 0 and shift < N:
+                        place = (shift // BLK - EARLY_A) % PERIOD
+                        nc.gpsimd.tensor_copy(out=diagonal[:, :, place : place + 1], in_=coefs[:, :, j : j + 1])
+            parked = out[0].rearrange("c n -> (c n)")
+            nc.sync.dma_start(
+                out=parked[0 : H * P * PERIOD].rearrange("(h r c) -> r h c", h=H, c=PERIOD), in_=diagonal[:]
+            )
             for h in range(H):
-                nc.vector.tensor_scalar_mul(
-                    out=toeplitz[:, h, :], in0=shifted[:, PAD + EARLY_A : PAD + P], scalar1=TAP3
-                )
-            for index in range(len(taps_of(0))):
-                for h in range(H):
-                    shift, coef = taps_of(h)[index]
-                    if shift % BLK == 0:
-                        first = PAD + EARLY_A - shift // BLK
-                        nc.vector.scalar_tensor_tensor(
-                            out=toeplitz[:, h, :],
-                            in0=shifted[:, first : first + LATE_A],
-                            scalar=coef,
-                            in1=toeplitz[:, h, :],
-                            op0=ALU.mult,
-                            op1=ALU.add,
-                        )
+                rows = parked[h * P * PERIOD : h * P * PERIOD + P * (PERIOD - 1)].rearrange("(r c) -> r c", c=PERIOD - 1)
+                nc.sync.dma_start(out=toeplitz[:, h, 0:LATE_A], in_=rows[:, 0:LATE_A])
 
         def add_tap(acc, f_t, shift, coef, first, last):
             nc.vector.scalar_tensor_tensor(
@@ -243,28 +252,40 @@ def tile_causalwaveletfieldattentionbyte_pa_t_kernel(
                 op1=ALU.add,
             )
 
-        def filter_head(pair, h):
-            field = fields[pair]
-            for b in range(BLK):
-                for member in range(PAIR):
-                    nc.scalar.activation(
-                        out=field[:, b, h, member, :],
-                        in_=field[:, b, h, member, :],
-                        func=ACT.Copy,
-                        scale=norms[pair][:, member, b, h : h + 1],
-                    )
+        def head_tiles():
             f_ab = work.tile([P, P, BLK], F32, bufs=2)
             acc_ab = work.tile([P, P, BLK], F32, bufs=3)
-            for g in range(CHUNKS):
+            return f_ab, acc_ab
+
+        def turn_tiles(pair, h, f_ab, acc_ab, groups, by_vector):
+            field = fields[pair]
+            for g in groups:
+                tiles = slice(g * TILES, (g + 1) * TILES)
+                if by_vector:
+                    f = field[:, tiles, h, :, :]
+                    m = norms[pair][:, :, tiles, h : h + 1].rearrange("p m b o -> p b m o")
+                    nc.vector.tensor_tensor(out=f, in0=f, in1=m.to_broadcast([P, TILES, PAIR, HD]), op=ALU.mult)
+                else:
+                    for b in range(tiles.start, tiles.stop):
+                        for member in range(PAIR):
+                            nc.scalar.activation(
+                                out=field[:, b, h, member, :],
+                                in_=field[:, b, h, member, :],
+                                func=ACT.Copy,
+                                scale=norms[pair][:, member, b, h : h + 1],
+                            )
+            for g in groups:
                 f_ps = psum.tile([P, TILES, P], F32)
                 late_ps = psum.tile([P, TILES, LATE_A], F32)
                 for i in range(TILES):
                     block = field[:, g * TILES + i, h, :, :].rearrange("p m c -> p (m c)")
                     nc.tensor.transpose(out=f_ps[:, i, :], in_=block, identity=identity)
-                    nc.tensor.matmul(out=late_ps[:, i, :], lhsT=block, rhs=toeplitz[:, h, :], start=True, stop=True)
+                    nc.tensor.matmul(out=late_ps[:, i, :], lhsT=block, rhs=toeplitz[:, h, 0:LATE_A], start=True, stop=True)
                 cols = slice(g * TILES, (g + 1) * TILES)
                 nc.scalar.copy(out=f_ab[:, :, cols], in_=f_ps[:].rearrange("p i a -> p a i"))
                 nc.scalar.copy(out=acc_ab[:, EARLY_A:P, cols], in_=late_ps[:].rearrange("p i a -> p a i"))
+
+        def filter_head(pair, h, f_ab, acc_ab):
             f_t = f_ab[:].rearrange("p a b -> p (a b)")
             acc = acc_ab[:].rearrange("p a b -> p (a b)")
             nc.scalar.mul(out=acc[:, 0:EARLY], in_=f_t[:, 0:EARLY], mul=TAP3)
@@ -285,26 +306,45 @@ def tile_causalwaveletfieldattentionbyte_pa_t_kernel(
                         in_=acc[member * HD : (member + 1) * HD, first:last],
                     )
 
-        def prepare(pair, chunks):
+        def prepare(pair, chunks, after):
             for step in range(len(chunks) + 1):
                 if step < len(chunks):
                     quantise_chunk(pair, chunks[step])
                 if step > 0:
                     value_chunk(pair, chunks[step - 1])
                     norm_chunk(pair, chunks[step - 1], 0)
+                    after(step - 1)
+
+        def whole_head(pair, h):
+            f_ab, acc_ab = head_tiles()
+            turn_tiles(pair, h, f_ab, acc_ab, range(CHUNKS), False)
+            filter_head(pair, h, f_ab, acc_ab)
+
+        def nothing(step):
+            return None
 
         chunks = PAIR * CHUNKS
-        prepare(0, range(chunks))
         build_toeplitz()
+        for index in range(chunks, B * CHUNKS):
+            x_chunks[index] = load_x_chunk(index)
+        first_f, first_acc = head_tiles()
+
+        def first_head(step):
+            if step % PAIR == PAIR - 1:
+                turn_tiles(0, 0, first_f, first_acc, [step // PAIR], True)
+
+        prepare(0, by_turns, first_head)
+        filter_head(0, 0, first_f, first_acc)
         for pair in range(B // PAIR):
             more = pair + 1 < B // PAIR
-            filter_head(pair, 0)
+            if pair > 0:
+                whole_head(pair, 0)
             for chunk in range(chunks):
                 norm_chunk(pair, chunk, 1)
-            filter_head(pair, 1)
+            whole_head(pair, 1)
             if more:
-                prepare(pair + 1, range(0, chunks // 2))
-            filter_head(pair, 2)
+                prepare(pair + 1, list(range(0, chunks // 2)), nothing)
+            whole_head(pair, 2)
             if more:
-                prepare(pair + 1, range(chunks // 2, chunks))
-            filter_head(pair, 3)
+                prepare(pair + 1, list(range(chunks // 2, chunks)), nothing)
+            whole_head(pair, 3)

@@ -285,7 +285,7 @@ def tile_causalwaveletfieldattentionbyte_pa_t_kernel(
                 nc.scalar.copy(out=f_ab[:, :, cols], in_=f_ps[:].rearrange("p i a -> p a i"))
                 nc.scalar.copy(out=acc_ab[:, EARLY_A:P, cols], in_=late_ps[:].rearrange("p i a -> p a i"))
 
-        def filter_head(pair, h, f_ab, acc_ab):
+        def filter_head(pair, h, f_ab, acc_ab, beside):
             f_t = f_ab[:].rearrange("p a b -> p (a b)")
             acc = acc_ab[:].rearrange("p a b -> p (a b)")
             nc.scalar.mul(out=acc[:, 0:EARLY], in_=f_t[:, 0:EARLY], mul=TAP3)
@@ -299,6 +299,8 @@ def tile_causalwaveletfieldattentionbyte_pa_t_kernel(
                 if k < len(late):
                     (shift, coef), first = late[k]
                     add_tap(acc, f_t, shift, coef, first, first + LATE_HALF)
+                for task in beside[len(beside) * k // len(early) : len(beside) * (k + 1) // len(early)]:
+                    task()
             for first, last in ((EARLY, EARLY + LATE_HALF), (EARLY + LATE_HALF, N), (0, EARLY)):
                 for member in range(PAIR):
                     nc.sync.dma_start(
@@ -315,13 +317,20 @@ def tile_causalwaveletfieldattentionbyte_pa_t_kernel(
                     norm_chunk(pair, chunks[step - 1], 0)
                     after(step - 1)
 
-        def whole_head(pair, h):
+        def whole_head(pair, h, beside):
             f_ab, acc_ab = head_tiles()
             turn_tiles(pair, h, f_ab, acc_ab, range(CHUNKS), False)
-            filter_head(pair, h, f_ab, acc_ab)
+            filter_head(pair, h, f_ab, acc_ab, beside)
 
         def nothing(step):
             return None
+
+        def prepare_step(pair, step):
+            if step < chunks:
+                quantise_chunk(pair, step)
+            if step > 0:
+                value_chunk(pair, step - 1)
+                norm_chunk(pair, step - 1, 0)
 
         chunks = PAIR * CHUNKS
         build_toeplitz()
@@ -334,17 +343,15 @@ def tile_causalwaveletfieldattentionbyte_pa_t_kernel(
                 turn_tiles(0, 0, first_f, first_acc, [step // PAIR], True)
 
         prepare(0, by_turns, first_head)
-        filter_head(0, 0, first_f, first_acc)
         for pair in range(B // PAIR):
-            more = pair + 1 < B // PAIR
-            if pair > 0:
-                whole_head(pair, 0)
-            for chunk in range(chunks):
-                norm_chunk(pair, chunk, 1)
-            whole_head(pair, 1)
-            if more:
-                prepare(pair + 1, list(range(0, chunks // 2)), nothing)
-            whole_head(pair, 2)
-            if more:
-                prepare(pair + 1, list(range(chunks // 2, chunks)), nothing)
-            whole_head(pair, 3)
+            second_halves = [lambda chunk=chunk: norm_chunk(pair, chunk, 1) for chunk in range(chunks)]
+            steps = [lambda step=step: prepare_step(pair + 1, step) for step in range(chunks + 1)]
+            if pair + 1 == B // PAIR:
+                steps = []
+            if pair == 0:
+                filter_head(0, 0, first_f, first_acc, second_halves)
+            else:
+                whole_head(pair, 0, second_halves)
+            whole_head(pair, 1, steps[0 : len(steps) // 2])
+            whole_head(pair, 2, steps[len(steps) // 2 :])
+            whole_head(pair, 3, [])

@@ -168,7 +168,7 @@ def tile_causalwaveletfieldattentionbyte_pa_t_kernel(
             member, g = divmod(chunk, CHUNKS)
             x_codes, x_plane = quantised[(pair, chunk)]
             for j in range(TILES // 2):
-                v_ps = psum.tile([P, 2, H, HD], F32)
+                v_ps = psum.tile([P, 2, H, HD], F32, bufs=2)
                 for t in range(2):
                     cols = slice((2 * j + t) * P, (2 * j + t + 1) * P)
                     nc.tensor.matmul_mx(
@@ -192,7 +192,7 @@ def tile_causalwaveletfieldattentionbyte_pa_t_kernel(
             member, g = divmod(chunk, CHUNKS)
             x_codes, x_plane = quantised[(pair, chunk)]
             cols = slice(half * P, (half + 1) * P)
-            k_ps = psum.tile([P, CHUNK], F32, bufs=2)
+            k_ps = psum.tile([P, CHUNK], F32)
             nc.tensor.matmul_mx(
                 out=k_ps[:],
                 lhsT=k_words[:, cols].bitcast(FP8X4),
@@ -284,11 +284,11 @@ def tile_causalwaveletfieldattentionbyte_pa_t_kernel(
                 cols = slice(g * TILES, (g + 1) * TILES)
                 nc.scalar.copy(out=f_ab[:, :, cols], in_=f_ps[:].rearrange("p i a -> p a i"))
                 nc.scalar.copy(out=acc_ab[:, EARLY_A:P, cols], in_=late_ps[:].rearrange("p i a -> p a i"))
+                nc.scalar.mul(out=acc_ab[:, 0:EARLY_A, cols], in_=f_ps[:, :, 0:EARLY_A].rearrange("p i a -> p a i"), mul=TAP3)
 
         def filter_head(pair, h, f_ab, acc_ab, beside):
             f_t = f_ab[:].rearrange("p a b -> p (a b)")
             acc = acc_ab[:].rearrange("p a b -> p (a b)")
-            nc.scalar.mul(out=acc[:, 0:EARLY], in_=f_t[:, 0:EARLY], mul=TAP3)
 
             taps = taps_of(h)
             early = [tap for tap in taps if tap[0] < EARLY]
@@ -317,11 +317,6 @@ def tile_causalwaveletfieldattentionbyte_pa_t_kernel(
                     norm_chunk(pair, chunks[step - 1], 0)
                     after(step - 1)
 
-        def whole_head(pair, h, beside):
-            f_ab, acc_ab = head_tiles()
-            turn_tiles(pair, h, f_ab, acc_ab, range(CHUNKS), False)
-            filter_head(pair, h, f_ab, acc_ab, beside)
-
         def nothing(step):
             return None
 
@@ -336,22 +331,26 @@ def tile_causalwaveletfieldattentionbyte_pa_t_kernel(
         build_toeplitz()
         for index in range(chunks, B * CHUNKS):
             x_chunks[index] = load_x_chunk(index)
-        first_f, first_acc = head_tiles()
+        heads = [(pair, h) for pair in range(B // PAIR) for h in range(H)]
+        turned = {0: head_tiles()}
 
         def first_head(step):
             if step % PAIR == PAIR - 1:
-                turn_tiles(0, 0, first_f, first_acc, [step // PAIR], True)
+                turn_tiles(0, 0, turned[0][0], turned[0][1], [step // PAIR], True)
 
+        def second_halves(pair):
+            return [lambda chunk=chunk: norm_chunk(pair, chunk, 1) for chunk in range(chunks)]
+
+        steps = [lambda step=step: prepare_step(1, step) for step in range(chunks + 1)]
+        beside = {
+            0: second_halves(0),
+            1: steps[0 : len(steps) // 2],
+            2: steps[len(steps) // 2 :],
+            H: second_halves(1),
+        }
         prepare(0, by_turns, first_head)
-        for pair in range(B // PAIR):
-            second_halves = [lambda chunk=chunk: norm_chunk(pair, chunk, 1) for chunk in range(chunks)]
-            steps = [lambda step=step: prepare_step(pair + 1, step) for step in range(chunks + 1)]
-            if pair + 1 == B // PAIR:
-                steps = []
-            if pair == 0:
-                filter_head(0, 0, first_f, first_acc, second_halves)
-            else:
-                whole_head(pair, 0, second_halves)
-            whole_head(pair, 1, steps[0 : len(steps) // 2])
-            whole_head(pair, 2, steps[len(steps) // 2 :])
-            whole_head(pair, 3, [])
+        for u in range(len(heads)):
+            if u + 1 < len(heads):
+                turned[u + 1] = head_tiles()
+                turn_tiles(heads[u + 1][0], heads[u + 1][1], turned[u + 1][0], turned[u + 1][1], range(CHUNKS), False)
+            filter_head(heads[u][0], heads[u][1], turned[u][0], turned[u][1], beside.get(u, []))

@@ -26,8 +26,6 @@ PAIR = 2
 EARLY_A = 28
 EARLY = EARLY_A * BLK
 LATE_A = P - EARLY_A
-MAX_SHIFT_A = 3 * 2 ** (NS - 2) // BLK
-PAD = MAX_SHIFT_A - EARLY_A
 LATE_HALF = (N - EARLY) // 2
 PERIOD = LATE_A + P - 1
 PITCH = 104
@@ -84,10 +82,9 @@ def tile_causalwaveletfieldattentionbyte_pa_t_kernel(
         nc.vector.memset(kb_rows[:], 0.0)
         nc.scalar.dma_start(out=kb_rows[0:2, :], in_=k_b.rearrange("(r c) -> r c", r=2))
 
-        shifted = const.tile([P, PAD + P], F32)
-        nc.gpsimd.memset(shifted[:, 0:PAD], 0.0)
-        make_identity(nc, shifted[:, PAD : PAD + P])
-        identity = shifted[:, PAD : PAD + P]
+        identity_tile = const.tile([P, P], F32)
+        make_identity(nc, identity_tile[:])
+        identity = identity_tile[:]
 
         head_of = const.tile([P, 2], F32)
         nc.vector.memset(head_of[:], 0.0)
@@ -308,47 +305,35 @@ def tile_causalwaveletfieldattentionbyte_pa_t_kernel(
                         in_=acc[member * HD : (member + 1) * HD, first:last],
                     )
 
-        def prepare(pair, chunks, after):
-            for step in range(len(chunks) + 1):
-                if step < len(chunks):
-                    quantise_chunk(pair, chunks[step])
-                if step > 0:
-                    value_chunk(pair, chunks[step - 1])
-                    norm_chunk(pair, chunks[step - 1], 0)
-                    after(step - 1)
-
-        def nothing(step):
-            return None
-
-        def prepare_step(pair, step):
-            if step < chunks:
-                quantise_chunk(pair, step)
+        def prepare_step(pair, order, step):
+            if step < len(order):
+                quantise_chunk(pair, order[step])
             if step > 0:
-                value_chunk(pair, step - 1)
-                norm_chunk(pair, step - 1, 0)
+                value_chunk(pair, order[step - 1])
+                norm_chunk(pair, order[step - 1], 0)
 
-        chunks = PAIR * CHUNKS
+        def second_halves(pair):
+            return [lambda chunk=chunk: norm_chunk(pair, chunk, 1) for chunk in range(PAIR * CHUNKS)]
+
         build_toeplitz()
-        for index in range(chunks, B * CHUNKS):
+        for index in range(PAIR * CHUNKS, B * CHUNKS):
             x_chunks[index] = load_x_chunk(index)
         heads = [(pair, h) for pair in range(B // PAIR) for h in range(H)]
         turned = {0: head_tiles()}
 
-        def first_head(step):
-            if step % PAIR == PAIR - 1:
-                turn_tiles(0, 0, turned[0][0], turned[0][1], [step // PAIR], True)
+        for step in range(len(by_turns) + 1):
+            prepare_step(0, by_turns, step)
+            if step > 0 and step % PAIR == 0:
+                turn_tiles(0, 0, turned[0][0], turned[0][1], [step // PAIR - 1], True)
 
-        def second_halves(pair):
-            return [lambda chunk=chunk: norm_chunk(pair, chunk, 1) for chunk in range(chunks)]
-
-        steps = [lambda step=step: prepare_step(1, step) for step in range(chunks + 1)]
+        in_order = list(range(PAIR * CHUNKS))
+        steps = [lambda step=step: prepare_step(1, in_order, step) for step in range(len(in_order) + 1)]
         beside = {
             0: second_halves(0),
             1: steps[0 : len(steps) // 2],
             2: steps[len(steps) // 2 :],
             H: second_halves(1),
         }
-        prepare(0, by_turns, first_head)
         for u in range(len(heads)):
             if u + 1 < len(heads):
                 turned[u + 1] = head_tiles()

@@ -28,6 +28,7 @@ EARLY = EARLY_A * BLK
 LATE_A = P - EARLY_A
 LATE_HALF = (N - EARLY) // 2
 PERIOD = LATE_A + P - 1
+PE_SHIFTS = {4: (1, 2), 5: (1, 2), 6: (1, 2), 7: (1, 2)}
 PITCH = 104
 
 FLOPS = 2 * B * N * D * 2 * C
@@ -127,6 +128,23 @@ def tile_causalwaveletfieldattentionbyte_pa_t_kernel(
         )
         coef_tri = const.tile([P, H, NS], F32)
         nc.vector.tensor_scalar_mul(out=coef_tri[:], in0=gain[:], scalar1=TAP0)
+
+        shift_one = const.tile([P, P], F32)
+        nc.vector.tensor_copy(out=shift_one[:, 1:P], in_=identity[:, 0 : P - 1])
+        nc.vector.tensor_copy(out=shift_one[:, 0:1], in_=identity[:, P - 1 : P])
+        not_last = const.tile([P, 1], F32)
+        nc.vector.tensor_scalar(
+            out=not_last[:], in0=identity[:, P - 1 : P], scalar1=-1.0, scalar2=1.0, op0=ALU.mult, op1=ALU.add
+        )
+        coef_pow_cut = const.tile([P, H, NS], F32)
+        nc.vector.tensor_scalar_mul(out=coef_pow_cut[:], in0=coef_pow[:], scalar1=not_last[:, 0:1])
+        coef_tri_cut = const.tile([P, H, NS], F32)
+        nc.vector.tensor_scalar_mul(out=coef_tri_cut[:], in0=coef_tri[:], scalar1=not_last[:, 0:1])
+
+        def coefs_of(h, shift):
+            j = [j for j in range(NS) if shift in (2**j, 3 * 2**j)][0]
+            whole, cut = (coef_pow, coef_pow_cut) if shift == 2**j else (coef_tri, coef_tri_cut)
+            return whole[:, h, j : j + 1], cut[:, h, j : j + 1]
 
         def taps_of(h):
             taps = [(2**j, coef_pow[:, h, j : j + 1]) for j in range(NS)]
@@ -254,8 +272,9 @@ def tile_causalwaveletfieldattentionbyte_pa_t_kernel(
             acc_ab = work.tile([P, P, BLK], F32, bufs=3)
             return f_ab, acc_ab
 
-        def turn_tiles(pair, h, f_ab, acc_ab, groups, by_vector):
+        def turn_tiles(pair, h, f_ab, acc_ab, groups, by_vector, shifts=()):
             field = fields[pair]
+            scaled = work.tile([P, max(len(shifts), 1), BLK, PAIR * HD], F32, bufs=1, tag="scaled")
             for g in groups:
                 tiles = slice(g * TILES, (g + 1) * TILES)
                 if by_vector:
@@ -271,24 +290,50 @@ def tile_causalwaveletfieldattentionbyte_pa_t_kernel(
                                 func=ACT.Copy,
                                 scale=norms[pair][:, member, b, h : h + 1],
                             )
+            for k, shift in enumerate(shifts):
+                whole, cut = coefs_of(h, shift)
+                for first, last, coef in ((0, BLK - shift, whole), (BLK - shift, BLK, cut)):
+                    nc.scalar.activation(
+                        out=scaled[:, k, first:last, :],
+                        in_=field[:, first:last, h, :, :].rearrange("p b m c -> p b (m c)"),
+                        func=ACT.Copy,
+                        scale=coef,
+                    )
             for g in groups:
                 f_ps = psum.tile([P, TILES, P], F32)
-                late_ps = psum.tile([P, TILES, LATE_A], F32)
+                late_ps = psum.tile([P, TILES, P], F32)
                 for i in range(TILES):
-                    block = field[:, g * TILES + i, h, :, :].rearrange("p m c -> p (m c)")
+                    b = g * TILES + i
+                    block = field[:, b, h, :, :].rearrange("p m c -> p (m c)")
                     nc.tensor.transpose(out=f_ps[:, i, :], in_=block, identity=identity)
-                    nc.tensor.matmul(out=late_ps[:, i, :], lhsT=block, rhs=toeplitz[:, h, 0:LATE_A], start=True, stop=True)
+                    for k, shift in enumerate(shifts):
+                        nc.tensor.matmul(
+                            out=late_ps[:, i, :],
+                            lhsT=scaled[:, k, (b - shift) % BLK, :],
+                            rhs=identity if b >= shift else shift_one[:],
+                            start=k == 0,
+                            stop=False,
+                            is_transpose=True,
+                        )
+                    nc.tensor.matmul(
+                        out=late_ps[:, i, EARLY_A:P], lhsT=block, rhs=toeplitz[:, h, 0:LATE_A], start=not shifts, stop=True
+                    )
                 cols = slice(g * TILES, (g + 1) * TILES)
                 nc.scalar.copy(out=f_ab[:, :, cols], in_=f_ps[:].rearrange("p i a -> p a i"))
-                nc.scalar.copy(out=acc_ab[:, EARLY_A:P, cols], in_=late_ps[:].rearrange("p i a -> p a i"))
-                nc.scalar.mul(out=acc_ab[:, 0:EARLY_A, cols], in_=f_ps[:, :, 0:EARLY_A].rearrange("p i a -> p a i"), mul=TAP3)
+                if shifts:
+                    nc.scalar.copy(out=acc_ab[:, :, cols], in_=late_ps[:].rearrange("p i a -> p a i"))
+                else:
+                    nc.scalar.copy(out=acc_ab[:, EARLY_A:P, cols], in_=late_ps[:, :, EARLY_A:P].rearrange("p i a -> p a i"))
+                    nc.scalar.mul(out=acc_ab[:, 0:EARLY_A, cols], in_=f_ps[:, :, 0:EARLY_A].rearrange("p i a -> p a i"), mul=TAP3)
 
-        def filter_head(pair, h, f_ab, acc_ab, beside):
+        def filter_head(pair, h, f_ab, acc_ab, beside, shifts=()):
             f_t = f_ab[:].rearrange("p a b -> p (a b)")
             acc = acc_ab[:].rearrange("p a b -> p (a b)")
 
-            taps = taps_of(h)
+            taps = [tap for tap in taps_of(h) if tap[0] not in shifts]
             early = [tap for tap in taps if tap[0] < EARLY]
+            if shifts:
+                early = [(0, TAP3)] + early
             late = [(tap, first) for tap in taps if tap[0] % BLK != 0 for first in (EARLY, EARLY + LATE_HALF)]
             for k in range(len(early)):
                 shift, coef = early[k]
@@ -337,5 +382,8 @@ def tile_causalwaveletfieldattentionbyte_pa_t_kernel(
         for u in range(len(heads)):
             if u + 1 < len(heads):
                 turned[u + 1] = head_tiles()
-                turn_tiles(heads[u + 1][0], heads[u + 1][1], turned[u + 1][0], turned[u + 1][1], range(CHUNKS), False)
-            filter_head(heads[u][0], heads[u][1], turned[u][0], turned[u][1], beside.get(u, []))
+                turn_tiles(
+                    heads[u + 1][0], heads[u + 1][1], turned[u + 1][0], turned[u + 1][1], range(CHUNKS), False,
+                    PE_SHIFTS.get(u + 1, ()),
+                )
+            filter_head(heads[u][0], heads[u][1], turned[u][0], turned[u][1], beside.get(u, []), PE_SHIFTS.get(u, ()))

@@ -28,7 +28,7 @@ EARLY = EARLY_A * BLK
 LATE_A = P - EARLY_A
 LATE_HALF = (N - EARLY) // 2
 PERIOD = LATE_A + P - 1
-PE_SHIFTS = {4: (1, 2), 5: (1, 2), 6: (1, 2), 7: (1, 2)}
+PE_SHIFTS = {1: (1, 2), 2: (1, 2), 3: (1, 2), 4: (1, 2), 5: (1, 2), 6: (1, 2), 7: (1, 2)}
 PITCH = 104
 
 FLOPS = 2 * B * N * D * 2 * C

@@ -23,13 +23,14 @@ TILES = 4
 CHUNK = TILES * P
 CHUNKS = BLK // TILES
 PAIR = 2
-EARLY_A = 28
+BY_VECTOR = 2
+EARLY_A = 22
 EARLY = EARLY_A * BLK
 LATE_A = P - EARLY_A
 LATE_HALF = (N - EARLY) // 2
 PERIOD = LATE_A + P - 1
 PE_SHIFTS = {1: (1, 2), 2: (1, 2), 3: (1, 2), 4: (1, 2), 5: (1, 2), 6: (1, 2), 7: (1, 2)}
-PITCH = 104
+PITCH = 112
 
 FLOPS = 2 * B * N * D * 2 * C
 
@@ -53,7 +54,7 @@ def tile_causalwaveletfieldattentionbyte_pa_t_kernel(
 
         def load_x_chunk(index):
             batch, g = divmod(index, CHUNKS)
-            x_chunk = const.tile([P, TILES, D], BF16, name="x%d" % index)
+            x_chunk = const.tile([P, TILES, D], BF16, tag="x_chunk", bufs=PAIR * CHUNKS)
             rows = x[batch].rearrange("(a b) k -> a b k", b=BLK)
             nc.sync.dma_start(out=x_chunk[:], in_=rows[:, g * TILES : (g + 1) * TILES, :])
             return x_chunk
@@ -267,14 +268,35 @@ def tile_causalwaveletfieldattentionbyte_pa_t_kernel(
                 op1=ALU.add,
             )
 
+        def add_rows(acc_ab, f_ab, rows, coef, first, last, cols):
+            nc.vector.scalar_tensor_tensor(
+                out=acc_ab[:, first:last, cols],
+                in0=f_ab[:, first - rows : last - rows, cols],
+                scalar=coef,
+                in1=acc_ab[:, first:last, cols],
+                op0=ALU.mult,
+                op1=ALU.add,
+            )
+
+        def group_adds(h, f_ab, acc_ab, g):
+            cols = slice(g * TILES, (g + 1) * TILES)
+            spans = [
+                (shift // BLK, coef, first, last)
+                for shift, coef in taps_of(h)
+                if shift % BLK == 0
+                for first, last in ((shift // BLK, P // 2), (max(shift // BLK, P // 2), P))
+                if first < last
+            ]
+            return [lambda span=span: add_rows(acc_ab, f_ab, span[0], span[1], span[2], span[3], cols) for span in spans]
+
         def head_tiles():
-            f_ab = work.tile([P, P, BLK], F32, bufs=2)
-            acc_ab = work.tile([P, P, BLK], F32, bufs=3)
+            f_ab = work.tile([P, P, BLK], F32, bufs=3)
+            acc_ab = work.tile([P, P, BLK], F32, bufs=4)
             return f_ab, acc_ab
 
-        def turn_tiles(pair, h, f_ab, acc_ab, groups, by_vector, shifts=()):
+        def turn_tiles(pair, h, f_ab, acc_ab, groups, by_vector, shifts=(), filtered=True):
             field = fields[pair]
-            scaled = work.tile([P, max(len(shifts), 1), BLK, PAIR * HD], F32, bufs=1, tag="scaled")
+            scaled = work.tile([P, max(len(shifts), 1), BLK, PAIR * HD], F32, bufs=2, tag="scaled")
             for g in groups:
                 tiles = slice(g * TILES, (g + 1) * TILES)
                 if by_vector:
@@ -301,7 +323,9 @@ def tile_causalwaveletfieldattentionbyte_pa_t_kernel(
                     )
             for g in groups:
                 f_ps = psum.tile([P, TILES, P], F32)
-                late_ps = psum.tile([P, TILES, P], F32)
+                late_ps = None
+                if filtered:
+                    late_ps = psum.tile([P, TILES, P], F32)
                 for i in range(TILES):
                     b = g * TILES + i
                     block = field[:, b, h, :, :].rearrange("p m c -> p (m c)")
@@ -315,18 +339,21 @@ def tile_causalwaveletfieldattentionbyte_pa_t_kernel(
                             stop=False,
                             is_transpose=True,
                         )
-                    nc.tensor.matmul(
-                        out=late_ps[:, i, EARLY_A:P], lhsT=block, rhs=toeplitz[:, h, 0:LATE_A], start=not shifts, stop=True
-                    )
+                    if filtered:
+                        nc.tensor.matmul(
+                            out=late_ps[:, i, EARLY_A:P], lhsT=block, rhs=toeplitz[:, h, 0:LATE_A], start=not shifts, stop=True
+                        )
                 cols = slice(g * TILES, (g + 1) * TILES)
                 nc.scalar.copy(out=f_ab[:, :, cols], in_=f_ps[:].rearrange("p i a -> p a i"))
                 if shifts:
                     nc.scalar.copy(out=acc_ab[:, :, cols], in_=late_ps[:].rearrange("p i a -> p a i"))
+                elif not filtered:
+                    nc.scalar.mul(out=acc_ab[:, :, cols], in_=f_ps[:].rearrange("p i a -> p a i"), mul=TAP3)
                 else:
                     nc.scalar.copy(out=acc_ab[:, EARLY_A:P, cols], in_=late_ps[:, :, EARLY_A:P].rearrange("p i a -> p a i"))
                     nc.scalar.mul(out=acc_ab[:, 0:EARLY_A, cols], in_=f_ps[:, :, 0:EARLY_A].rearrange("p i a -> p a i"), mul=TAP3)
 
-        def filter_head(pair, h, f_ab, acc_ab, beside, shifts=()):
+        def filter_head(pair, h, f_ab, acc_ab, beside, shifts=(), done_groups=0):
             f_t = f_ab[:].rearrange("p a b -> p (a b)")
             acc = acc_ab[:].rearrange("p a b -> p (a b)")
 
@@ -337,7 +364,10 @@ def tile_causalwaveletfieldattentionbyte_pa_t_kernel(
             late = [(tap, first) for tap in taps if tap[0] % BLK != 0 for first in (EARLY, EARLY + LATE_HALF)]
             for k in range(len(early)):
                 shift, coef = early[k]
-                add_tap(acc, f_t, shift, coef, shift, EARLY)
+                if shift > 0 and shift % BLK == 0 and done_groups > 0:
+                    add_rows(acc_ab, f_ab, shift // BLK, coef, shift // BLK, EARLY_A, slice(done_groups * TILES, BLK))
+                else:
+                    add_tap(acc, f_t, shift, coef, shift, EARLY)
                 if k < len(late):
                     (shift, coef), first = late[k]
                     add_tap(acc, f_t, shift, coef, first, first + LATE_HALF)
@@ -350,26 +380,40 @@ def tile_causalwaveletfieldattentionbyte_pa_t_kernel(
                         in_=acc[member * HD : (member + 1) * HD, first:last],
                     )
 
-        def prepare_step(pair, order, step):
+        def prepare_step(pair, order, step, fillers=()):
+            thirds = [fillers[len(fillers) * i // 3 : len(fillers) * (i + 1) // 3] for i in range(3)]
             if step < len(order):
                 quantise_chunk(pair, order[step])
+            for task in thirds[0]:
+                task()
             if step > 0:
                 value_chunk(pair, order[step - 1])
+            for task in thirds[1]:
+                task()
+            if step > 0:
                 norm_chunk(pair, order[step - 1], 0)
+            for task in thirds[2]:
+                task()
 
         def second_halves(pair):
             return [lambda chunk=chunk: norm_chunk(pair, chunk, 1) for chunk in range(PAIR * CHUNKS)]
 
         build_toeplitz()
-        for index in range(PAIR * CHUNKS, B * CHUNKS):
-            x_chunks[index] = load_x_chunk(index)
         heads = [(pair, h) for pair in range(B // PAIR) for h in range(H)]
         turned = {0: head_tiles()}
 
+        fillers = {}
         for step in range(len(by_turns) + 1):
-            prepare_step(0, by_turns, step)
+            prepare_step(0, by_turns, step, fillers.get(step, ()))
+            if step < len(by_turns):
+                x_chunks[PAIR * CHUNKS + step] = load_x_chunk(PAIR * CHUNKS + step)
             if step > 0 and step % PAIR == 0:
-                turn_tiles(0, 0, turned[0][0], turned[0][1], [step // PAIR - 1], True)
+                g = step // PAIR - 1
+                turn_tiles(0, 0, turned[0][0], turned[0][1], [g], True, (), g >= BY_VECTOR)
+                if g < BY_VECTOR:
+                    adds = group_adds(0, turned[0][0], turned[0][1], g)
+                    fillers[step + 1] = adds[0 : len(adds) // 2]
+                    fillers[step + 2] = adds[len(adds) // 2 :]
 
         in_order = list(range(PAIR * CHUNKS))
         steps = [lambda step=step: prepare_step(1, in_order, step) for step in range(len(in_order) + 1)]
@@ -386,4 +430,7 @@ def tile_causalwaveletfieldattentionbyte_pa_t_kernel(
                     heads[u + 1][0], heads[u + 1][1], turned[u + 1][0], turned[u + 1][1], range(CHUNKS), False,
                     PE_SHIFTS.get(u + 1, ()),
                 )
-            filter_head(heads[u][0], heads[u][1], turned[u][0], turned[u][1], beside.get(u, []), PE_SHIFTS.get(u, ()))
+            filter_head(
+                heads[u][0], heads[u][1], turned[u][0], turned[u][1], beside.get(u, []), PE_SHIFTS.get(u, ()),
+                BY_VECTOR if u == 0 else 0,
+            )

@@ -29,7 +29,7 @@ EARLY = EARLY_A * BLK
 LATE_A = P - EARLY_A
 LATE_HALF = (N - EARLY) // 2
 PERIOD = LATE_A + P - 1
-PE_SHIFTS = {1: (1, 2), 2: (1, 2), 3: (1, 2), 4: (1, 2), 5: (1, 2), 6: (1, 2), 7: (1, 2)}
+PE_SHIFTS = {4: (1, 2), 5: (1, 2), 6: (1, 2), 7: (1, 2)}
 PITCH = 112
 
 FLOPS = 2 * B * N * D * 2 * C

@@ -30,6 +30,7 @@ LATE_A = P - EARLY_A
 LATE_HALF = (N - EARLY) // 2
 PERIOD = LATE_A + P - 1
 PE_SHIFTS = {4: (1, 2), 5: (1, 2), 6: (1, 2), 7: (1, 2)}
+LAST_STEPS = 2
 PITCH = 112
 
 FLOPS = 2 * B * N * D * 2 * C
@@ -160,7 +161,7 @@ def tile_causalwaveletfieldattentionbyte_pa_t_kernel(
         def quantise_chunk(pair, chunk):
             x_chunk = x_chunks[pair * PAIR * CHUNKS + chunk]
 
-            grouped = stage.tile([P, CHUNK, PACK], BF16, align_bytes=64)
+            grouped = stage.tile([P, CHUNK, PACK], BF16, align_bytes=64, bufs=3)
             grouped_words = (
                 grouped[:].rearrange("p n t -> p (n t)").bitcast(F32).rearrange("p (i a u) -> p i a u", i=TILES, u=2)
             )
@@ -204,7 +205,7 @@ def tile_causalwaveletfieldattentionbyte_pa_t_kernel(
                     op=ALU.add,
                 )
 
-        def norm_chunk(pair, chunk, half):
+        def norm_chunk(pair, chunk, half, now=()):
             member, g = divmod(chunk, CHUNKS)
             x_codes, x_plane = quantised[(pair, chunk)]
             cols = slice(half * P, (half + 1) * P)
@@ -230,6 +231,8 @@ def tile_causalwaveletfieldattentionbyte_pa_t_kernel(
                 in_=m2_ps[:],
                 func=ACT.Sqrt,
             )
+            for h in now:
+                norm_by_scalar(pair, h, g, [member])
 
         toeplitz = const.tile([P, H, PITCH], F32)
 
@@ -294,64 +297,75 @@ def tile_causalwaveletfieldattentionbyte_pa_t_kernel(
             acc_ab = work.tile([P, P, BLK], F32, bufs=4)
             return f_ab, acc_ab
 
-        def turn_tiles(pair, h, f_ab, acc_ab, groups, by_vector, shifts=(), filtered=True):
-            field = fields[pair]
-            scaled = work.tile([P, max(len(shifts), 1), BLK, PAIR * HD], F32, bufs=2, tag="scaled")
-            for g in groups:
-                tiles = slice(g * TILES, (g + 1) * TILES)
-                if by_vector:
-                    f = field[:, tiles, h, :, :]
-                    m = norms[pair][:, :, tiles, h : h + 1].rearrange("p m b o -> p b m o")
-                    nc.vector.tensor_tensor(out=f, in0=f, in1=m.to_broadcast([P, TILES, PAIR, HD]), op=ALU.mult)
-                else:
-                    for b in range(tiles.start, tiles.stop):
-                        for member in range(PAIR):
-                            nc.scalar.activation(
-                                out=field[:, b, h, member, :],
-                                in_=field[:, b, h, member, :],
-                                func=ACT.Copy,
-                                scale=norms[pair][:, member, b, h : h + 1],
-                            )
-            for k, shift in enumerate(shifts):
-                whole, cut = coefs_of(h, shift)
-                for first, last, coef in ((0, BLK - shift, whole), (BLK - shift, BLK, cut)):
+        def norm_by_vector(pair, h, g):
+            tiles = slice(g * TILES, (g + 1) * TILES)
+            f = fields[pair][:, tiles, h, :, :]
+            m = norms[pair][:, :, tiles, h : h + 1].rearrange("p m b o -> p b m o")
+            nc.vector.tensor_tensor(out=f, in0=f, in1=m.to_broadcast([P, TILES, PAIR, HD]), op=ALU.mult)
+
+        def norm_by_scalar(pair, h, g, members):
+            for b in range(g * TILES, (g + 1) * TILES):
+                for member in members:
                     nc.scalar.activation(
-                        out=scaled[:, k, first:last, :],
-                        in_=field[:, first:last, h, :, :].rearrange("p b m c -> p b (m c)"),
+                        out=fields[pair][:, b, h, member, :],
+                        in_=fields[pair][:, b, h, member, :],
                         func=ACT.Copy,
-                        scale=coef,
+                        scale=norms[pair][:, member, b, h : h + 1],
                     )
-            for g in groups:
-                f_ps = psum.tile([P, TILES, P], F32)
-                late_ps = None
+
+        scaled_of = {}
+
+        def scale_head(u):
+            pair, h = heads[u]
+            shifts = PE_SHIFTS.get(u, ())
+            if shifts:
+                scaled = work.tile([P, len(shifts), BLK, PAIR * HD], F32, bufs=2)
+                scaled_of[u] = scaled
+                for k, shift in enumerate(shifts):
+                    whole, cut = coefs_of(h, shift)
+                    for first, last, coef in ((0, BLK - shift, whole), (BLK - shift, BLK, cut)):
+                        nc.scalar.activation(
+                            out=scaled[:, k, first:last, :],
+                            in_=fields[pair][:, first:last, h, :, :].rearrange("p b m c -> p b (m c)"),
+                            func=ACT.Copy,
+                            scale=coef,
+                        )
+
+        def turn_group(u, g, filtered=True):
+            pair, h = heads[u]
+            f_ab, acc_ab = turned[u]
+            shifts = PE_SHIFTS.get(u, ())
+            scaled = scaled_of.get(u)
+            f_ps = psum.tile([P, TILES, P], F32)
+            late_ps = None
+            if filtered:
+                late_ps = psum.tile([P, TILES, P], F32)
+            for i in range(TILES):
+                b = g * TILES + i
+                block = fields[pair][:, b, h, :, :].rearrange("p m c -> p (m c)")
+                nc.tensor.transpose(out=f_ps[:, i, :], in_=block, identity=identity)
+                for k, shift in enumerate(shifts):
+                    nc.tensor.matmul(
+                        out=late_ps[:, i, :],
+                        lhsT=scaled[:, k, (b - shift) % BLK, :],
+                        rhs=identity if b >= shift else shift_one[:],
+                        start=k == 0,
+                        stop=False,
+                        is_transpose=True,
+                    )
                 if filtered:
-                    late_ps = psum.tile([P, TILES, P], F32)
-                for i in range(TILES):
-                    b = g * TILES + i
-                    block = field[:, b, h, :, :].rearrange("p m c -> p (m c)")
-                    nc.tensor.transpose(out=f_ps[:, i, :], in_=block, identity=identity)
-                    for k, shift in enumerate(shifts):
-                        nc.tensor.matmul(
-                            out=late_ps[:, i, :],
-                            lhsT=scaled[:, k, (b - shift) % BLK, :],
-                            rhs=identity if b >= shift else shift_one[:],
-                            start=k == 0,
-                            stop=False,
-                            is_transpose=True,
-                        )
-                    if filtered:
-                        nc.tensor.matmul(
-                            out=late_ps[:, i, EARLY_A:P], lhsT=block, rhs=toeplitz[:, h, 0:LATE_A], start=not shifts, stop=True
-                        )
-                cols = slice(g * TILES, (g + 1) * TILES)
-                nc.scalar.copy(out=f_ab[:, :, cols], in_=f_ps[:].rearrange("p i a -> p a i"))
-                if shifts:
-                    nc.scalar.copy(out=acc_ab[:, :, cols], in_=late_ps[:].rearrange("p i a -> p a i"))
-                elif not filtered:
-                    nc.scalar.mul(out=acc_ab[:, :, cols], in_=f_ps[:].rearrange("p i a -> p a i"), mul=TAP3)
-                else:
-                    nc.scalar.copy(out=acc_ab[:, EARLY_A:P, cols], in_=late_ps[:, :, EARLY_A:P].rearrange("p i a -> p a i"))
-                    nc.scalar.mul(out=acc_ab[:, 0:EARLY_A, cols], in_=f_ps[:, :, 0:EARLY_A].rearrange("p i a -> p a i"), mul=TAP3)
+                    nc.tensor.matmul(
+                        out=late_ps[:, i, EARLY_A:P], lhsT=block, rhs=toeplitz[:, h, 0:LATE_A], start=not shifts, stop=True
+                    )
+            cols = slice(g * TILES, (g + 1) * TILES)
+            nc.scalar.copy(out=f_ab[:, :, cols], in_=f_ps[:].rearrange("p i a -> p a i"))
+            if shifts:
+                nc.scalar.copy(out=acc_ab[:, :, cols], in_=late_ps[:].rearrange("p i a -> p a i"))
+            elif not filtered:
+                nc.scalar.mul(out=acc_ab[:, :, cols], in_=f_ps[:].rearrange("p i a -> p a i"), mul=TAP3)
+            else:
+                nc.scalar.copy(out=acc_ab[:, EARLY_A:P, cols], in_=late_ps[:, :, EARLY_A:P].rearrange("p i a -> p a i"))
+                nc.scalar.mul(out=acc_ab[:, 0:EARLY_A, cols], in_=f_ps[:, :, 0:EARLY_A].rearrange("p i a -> p a i"), mul=TAP3)
 
         def filter_head(pair, h, f_ab, acc_ab, beside, shifts=(), done_groups=0):
             f_t = f_ab[:].rearrange("p a b -> p (a b)")
@@ -380,7 +394,7 @@ def tile_causalwaveletfieldattentionbyte_pa_t_kernel(
                         in_=acc[member * HD : (member + 1) * HD, first:last],
                     )
 
-        def prepare_step(pair, order, step, fillers=()):
+        def prepare_step(pair, order, step, fillers=(), now=()):
             thirds = [fillers[len(fillers) * i // 3 : len(fillers) * (i + 1) // 3] for i in range(3)]
             if step < len(order):
                 quantise_chunk(pair, order[step])
@@ -391,12 +405,12 @@ def tile_causalwaveletfieldattentionbyte_pa_t_kernel(
             for task in thirds[1]:
                 task()
             if step > 0:
-                norm_chunk(pair, order[step - 1], 0)
+                norm_chunk(pair, order[step - 1], 0, now)
             for task in thirds[2]:
                 task()
 
         def second_halves(pair):
-            return [lambda chunk=chunk: norm_chunk(pair, chunk, 1) for chunk in range(PAIR * CHUNKS)]
+            return [lambda chunk=chunk: norm_chunk(pair, chunk, 1, (2,)) for chunk in range(PAIR * CHUNKS)]
 
         build_toeplitz()
         heads = [(pair, h) for pair in range(B // PAIR) for h in range(H)]
@@ -409,28 +423,41 @@ def tile_causalwaveletfieldattentionbyte_pa_t_kernel(
                 x_chunks[PAIR * CHUNKS + step] = load_x_chunk(PAIR * CHUNKS + step)
             if step > 0 and step % PAIR == 0:
                 g = step // PAIR - 1
-                turn_tiles(0, 0, turned[0][0], turned[0][1], [g], True, (), g >= BY_VECTOR)
+                norm_by_vector(0, 0, g)
+                turn_group(0, g, g >= BY_VECTOR)
+                norm_by_scalar(0, 1, g, range(PAIR))
                 if g < BY_VECTOR:
                     adds = group_adds(0, turned[0][0], turned[0][1], g)
                     fillers[step + 1] = adds[0 : len(adds) // 2]
                     fillers[step + 2] = adds[len(adds) // 2 :]
 
         in_order = list(range(PAIR * CHUNKS))
-        steps = [lambda step=step: prepare_step(1, in_order, step) for step in range(len(in_order) + 1)]
+        steps = [lambda step=step: prepare_step(1, in_order, step, (), (0,)) for step in range(len(in_order) + 1)]
         beside = {
             0: second_halves(0),
-            1: steps[0 : len(steps) // 2],
-            2: steps[len(steps) // 2 :],
-            H: second_halves(1),
+            1: steps[0 : len(steps) // 2 + 1],
+            LAST_STEPS: steps[len(steps) // 2 + 1 :],
+            H - 1: second_halves(1),
         }
+        def turn_task(u, g):
+            turn_group(u, g)
+            if u + 1 < len(heads) and heads[u + 1][1] % 2 == 1:
+                norm_by_scalar(heads[u + 1][0], heads[u + 1][1], g, range(PAIR))
+
+        scale_head(1)
         for u in range(len(heads)):
+            tasks = beside.get(u, [])
             if u + 1 < len(heads):
                 turned[u + 1] = head_tiles()
-                turn_tiles(
-                    heads[u + 1][0], heads[u + 1][1], turned[u + 1][0], turned[u + 1][1], range(CHUNKS), False,
-                    PE_SHIFTS.get(u + 1, ()),
-                )
+                turning = [lambda u=u, g=g: turn_task(u + 1, g) for g in range(CHUNKS)]
+                if u == LAST_STEPS:
+                    tasks = tasks + turning + [lambda u=u: scale_head(u + 2)]
+                else:
+                    for task in turning:
+                        task()
             filter_head(
-                heads[u][0], heads[u][1], turned[u][0], turned[u][1], beside.get(u, []), PE_SHIFTS.get(u, ()),
+                heads[u][0], heads[u][1], turned[u][0], turned[u][1], tasks, PE_SHIFTS.get(u, ()),
                 BY_VECTOR if u == 0 else 0,
             )
+            if u + 2 < len(heads) and u != LAST_STEPS:
+                scale_head(u + 2)

@@ -29,7 +29,8 @@ EARLY = EARLY_A * BLK
 LATE_A = P - EARLY_A
 LATE_HALF = (N - EARLY) // 2
 PERIOD = LATE_A + P - 1
-PE_SHIFTS = {4: (1, 2), 5: (1, 2), 6: (1, 2), 7: (1, 2)}
+X_BUFS = 4
+PE_SHIFTS = {4: (1, 2), 5: (1, 2, 3), 6: (1, 2, 3, 4), 7: (1, 2, 3, 4)}
 LAST_STEPS = 2
 PITCH = 112
 
@@ -55,7 +56,7 @@ def tile_causalwaveletfieldattentionbyte_pa_t_kernel(
 
         def load_x_chunk(index):
             batch, g = divmod(index, CHUNKS)
-            x_chunk = const.tile([P, TILES, D], BF16, tag="x_chunk", bufs=PAIR * CHUNKS)
+            x_chunk = const.tile([P, TILES, D], BF16, tag="x_chunk", bufs=X_BUFS)
             rows = x[batch].rearrange("(a b) k -> a b k", b=BLK)
             nc.sync.dma_start(out=x_chunk[:], in_=rows[:, g * TILES : (g + 1) * TILES, :])
             return x_chunk
@@ -71,10 +72,11 @@ def tile_causalwaveletfieldattentionbyte_pa_t_kernel(
                 )
 
         by_turns = [member * CHUNKS + g for g in range(CHUNKS) for member in range(PAIR)]
-        x_chunks = {by_turns[0]: load_x_chunk(by_turns[0])}
+        x_order = by_turns + list(range(PAIR * CHUNKS, B * CHUNKS))
+        x_chunks = {x_order[0]: load_x_chunk(x_order[0])}
         load_weight(k_words, k_plane, k_w_words, k_w_scales)
         load_weight(v_words, v_plane, v_w_words, v_w_scales)
-        for index in by_turns[1:]:
+        for index in x_order[1:X_BUFS]:
             x_chunks[index] = load_x_chunk(index)
 
         gain_bf = const.tile([P, NS * H], BF16)
@@ -153,7 +155,7 @@ def tile_causalwaveletfieldattentionbyte_pa_t_kernel(
             taps += [(3 * 2**j, coef_tri[:, h, j : j + 1]) for j in range(NS)]
             return [tap for tap in taps if tap[0] < N]
 
-        fields = [const.tile([P, BLK, H, PAIR, HD], F32, name="field%d" % pair) for pair in range(B // PAIR)]
+        fields = [const.tile([P, BLK, H, PAIR, HD], F32, name="field%d" % pair, tag="field%d" % pair) for pair in range(B // PAIR)]
         norms = [const.tile([P, PAIR, BLK, H], F32, name="norm%d" % pair) for pair in range(B // PAIR)]
 
         quantised = {}
@@ -174,6 +176,9 @@ def tile_causalwaveletfieldattentionbyte_pa_t_kernel(
                 nc.scalar.copy(
                     out=grouped_words[:, 2 * j : 2 * j + 2, :, :], in_=x_ps[:].rearrange("p t u a -> p t a u")
                 )
+            place = x_order.index(pair * PAIR * CHUNKS + chunk) + X_BUFS
+            if place < len(x_order):
+                x_chunks[x_order[place]] = load_x_chunk(x_order[place])
             x_codes = stage.tile([P, CHUNK], U32, align_bytes=64, bufs=PAIR * CHUNKS)
             x_plane = stage.tile([P, CHUNK], U8, align_bytes=64, bufs=PAIR * CHUNKS)
             quantised[(pair, chunk)] = (x_codes, x_plane)
@@ -319,11 +324,16 @@ def tile_causalwaveletfieldattentionbyte_pa_t_kernel(
             pair, h = heads[u]
             shifts = PE_SHIFTS.get(u, ())
             if shifts:
-                scaled = work.tile([P, len(shifts), BLK, PAIR * HD], F32, bufs=2)
+                if u % 2 == 0:
+                    scaled = work.tile([P, len(shifts), BLK, PAIR * HD], F32, bufs=1)
+                else:
+                    scaled = const.tile([P, len(shifts), BLK, PAIR * HD], F32, tag="field0")
                 scaled_of[u] = scaled
                 for k, shift in enumerate(shifts):
                     whole, cut = coefs_of(h, shift)
-                    for first, last, coef in ((0, BLK - shift, whole), (BLK - shift, BLK, cut)):
+                    pieces = [(first, first + TILES, whole) for first in range(0, BLK - TILES, TILES)]
+                    pieces += [(BLK - TILES, BLK - shift, whole), (BLK - shift, BLK, cut)]
+                    for first, last, coef in [piece for piece in pieces if piece[0] < piece[1]]:
                         nc.scalar.activation(
                             out=scaled[:, k, first:last, :],
                             in_=fields[pair][:, first:last, h, :, :].rearrange("p b m c -> p b (m c)"),
@@ -336,14 +346,25 @@ def tile_causalwaveletfieldattentionbyte_pa_t_kernel(
             f_ab, acc_ab = turned[u]
             shifts = PE_SHIFTS.get(u, ())
             scaled = scaled_of.get(u)
-            f_ps = psum.tile([P, TILES, P], F32)
             late_ps = None
-            if filtered:
-                late_ps = psum.tile([P, TILES, P], F32)
+            if shifts:
+                f_ps = psum.tile([P, TILES, P], F32, tag="v_ps", bufs=2)
+                late_ps = psum.tile([P, TILES, P], F32, tag="x_ps", bufs=2)
+            else:
+                f_ps = psum.tile([P, TILES, P], F32)
+                if filtered:
+                    late_ps = psum.tile([P, TILES, P], F32)
+            cols = slice(g * TILES, (g + 1) * TILES)
+            for i in range(TILES):
+                block = fields[pair][:, g * TILES + i, h, :, :].rearrange("p m c -> p (m c)")
+                nc.tensor.transpose(out=f_ps[:, i, :], in_=block, identity=identity)
+            nc.scalar.copy(out=f_ab[:, :, cols], in_=f_ps[:].rearrange("p i a -> p a i"))
+            if not shifts:
+                plain = EARLY_A if filtered else P
+                nc.scalar.mul(out=acc_ab[:, 0:plain, cols], in_=f_ps[:, :, 0:plain].rearrange("p i a -> p a i"), mul=TAP3)
             for i in range(TILES):
                 b = g * TILES + i
                 block = fields[pair][:, b, h, :, :].rearrange("p m c -> p (m c)")
-                nc.tensor.transpose(out=f_ps[:, i, :], in_=block, identity=identity)
                 for k, shift in enumerate(shifts):
                     nc.tensor.matmul(
                         out=late_ps[:, i, :],
@@ -357,15 +378,10 @@ def tile_causalwaveletfieldattentionbyte_pa_t_kernel(
                     nc.tensor.matmul(
                         out=late_ps[:, i, EARLY_A:P], lhsT=block, rhs=toeplitz[:, h, 0:LATE_A], start=not shifts, stop=True
                     )
-            cols = slice(g * TILES, (g + 1) * TILES)
-            nc.scalar.copy(out=f_ab[:, :, cols], in_=f_ps[:].rearrange("p i a -> p a i"))
             if shifts:
                 nc.scalar.copy(out=acc_ab[:, :, cols], in_=late_ps[:].rearrange("p i a -> p a i"))
-            elif not filtered:
-                nc.scalar.mul(out=acc_ab[:, :, cols], in_=f_ps[:].rearrange("p i a -> p a i"), mul=TAP3)
-            else:
+            elif filtered:
                 nc.scalar.copy(out=acc_ab[:, EARLY_A:P, cols], in_=late_ps[:, :, EARLY_A:P].rearrange("p i a -> p a i"))
-                nc.scalar.mul(out=acc_ab[:, 0:EARLY_A, cols], in_=f_ps[:, :, 0:EARLY_A].rearrange("p i a -> p a i"), mul=TAP3)
 
         def filter_head(pair, h, f_ab, acc_ab, beside, shifts=(), done_groups=0):
             f_t = f_ab[:].rearrange("p a b -> p (a b)")
@@ -416,20 +432,18 @@ def tile_causalwaveletfieldattentionbyte_pa_t_kernel(
         heads = [(pair, h) for pair in range(B // PAIR) for h in range(H)]
         turned = {0: head_tiles()}
 
-        fillers = {}
+        fillers = []
         for step in range(len(by_turns) + 1):
-            prepare_step(0, by_turns, step, fillers.get(step, ()))
-            if step < len(by_turns):
-                x_chunks[PAIR * CHUNKS + step] = load_x_chunk(PAIR * CHUNKS + step)
+            prepare_step(0, by_turns, step)
             if step > 0 and step % PAIR == 0:
                 g = step // PAIR - 1
                 norm_by_vector(0, 0, g)
                 turn_group(0, g, g >= BY_VECTOR)
                 norm_by_scalar(0, 1, g, range(PAIR))
                 if g < BY_VECTOR:
-                    adds = group_adds(0, turned[0][0], turned[0][1], g)
-                    fillers[step + 1] = adds[0 : len(adds) // 2]
-                    fillers[step + 2] = adds[len(adds) // 2 :]
+                    fillers.extend(group_adds(0, turned[0][0], turned[0][1], g))
+        for task in fillers:
+            task()
 
         in_order = list(range(PAIR * CHUNKS))
         steps = [lambda step=step: prepare_step(1, in_order, step, (), (0,)) for step in range(len(in_order) + 1)]

@@ -391,17 +391,21 @@ def tile_causalwaveletfieldattentionbyte_pa_t_kernel(
             early = [tap for tap in taps if tap[0] < EARLY]
             if shifts:
                 early = [(0, TAP3)] + early
-            late = [(tap, first) for tap in taps if tap[0] % BLK != 0 for first in (EARLY, EARLY + LATE_HALF)]
-            for k in range(len(early)):
-                shift, coef = early[k]
-                if shift > 0 and shift % BLK == 0 and done_groups > 0:
-                    add_rows(acc_ab, f_ab, shift // BLK, coef, shift // BLK, EARLY_A, slice(done_groups * TILES, BLK))
-                else:
-                    add_tap(acc, f_t, shift, coef, shift, EARLY)
+            pieces = 3 if shifts else 2
+            bounds = [EARLY + BLK * (LATE_A * i // pieces) for i in range(pieces + 1)]
+            late = [(tap, i) for tap in taps if tap[0] % BLK != 0 for i in range(pieces)]
+            slots = max(len(early), len(late))
+            for k in range(slots):
+                if k < len(early):
+                    shift, coef = early[k]
+                    if shift > 0 and shift % BLK == 0 and done_groups > 0:
+                        add_rows(acc_ab, f_ab, shift // BLK, coef, shift // BLK, EARLY_A, slice(done_groups * TILES, BLK))
+                    else:
+                        add_tap(acc, f_t, shift, coef, shift, EARLY)
                 if k < len(late):
-                    (shift, coef), first = late[k]
-                    add_tap(acc, f_t, shift, coef, first, first + LATE_HALF)
-                for task in beside[len(beside) * k // len(early) : len(beside) * (k + 1) // len(early)]:
+                    (shift, coef), i = late[k]
+                    add_tap(acc, f_t, shift, coef, bounds[i], bounds[i + 1])
+                for task in beside[len(beside) * k // slots : len(beside) * (k + 1) // slots]:
                     task()
             for first, last in ((EARLY, EARLY + LATE_HALF), (EARLY + LATE_HALF, N), (0, EARLY)):
                 for member in range(PAIR):

from contextlib import ExitStack

import concourse.mybir as mybir
from concourse.masks import make_identity

F32 = mybir.dt.float32
BF16 = mybir.dt.bfloat16
I32 = mybir.dt.int32
U32 = mybir.dt.uint32
U8 = mybir.dt.uint8
FP8X4 = mybir.dt.float8_e4m3fn_x4
ALU = mybir.AluOpType
ACT = mybir.ActivationFunctionType

B, N, D, C, H, NS = 4, 2048, 512, 256, 4, 11
HD = C // H
TAP0, TAP1, TAP2, TAP3 = 0.4829629131445341, 0.8365163037378079, 0.2241438680420134, -0.1294095225512604

P = 128
PACK = 4
BLK = N // P
TILES = 4
CHUNK = TILES * P
CHUNKS = BLK // TILES
PAIR = 2
BY_VECTOR = 2
EARLY_A = 22
EARLY = EARLY_A * BLK
LATE_A = P - EARLY_A
LATE_HALF = (N - EARLY) // 2
PERIOD = LATE_A + P - 1
X_BUFS = 4
PE_SHIFTS = {4: (1, 2), 5: (1, 2, 3), 6: (1, 2, 3, 4), 7: (1, 2, 3, 4)}
LAST_STEPS = 2
PITCH = 112

FLOPS = 2 * B * N * D * 2 * C


def tile_causalwaveletfieldattentionbyte_pa_t_kernel(
    tc, x, k_w_words, k_w_scales, k_b, v_w_words, v_w_scales, v_b, scale_gain, out
):
    nc = tc.nc
    with ExitStack() as stack:
        const = stack.enter_context(tc.tile_pool(name="const", bufs=1))
        stage = stack.enter_context(tc.tile_pool(name="stage", bufs=2))
        work = stack.enter_context(tc.tile_pool(name="work", bufs=2))
        psum = stack.enter_context(tc.psum_pool(name="psum", bufs=1))

        k_plane = const.tile([P, C], U8, align_bytes=64)
        v_plane = const.tile([P, C], U8, align_bytes=64)
        nc.vector.memset(k_plane[:].bitcast(I32), 0)
        nc.vector.memset(v_plane[:].bitcast(I32), 0)
        k_words = const.tile([P, C], U32, align_bytes=64)
        v_words = const.tile([P, C], U32, align_bytes=64)

        def load_x_chunk(index):
            batch, g = divmod(index, CHUNKS)
            x_chunk = const.tile([P, TILES, D], BF16, tag="x_chunk", bufs=X_BUFS)
            rows = x[batch].rearrange("(a b) k -> a b k", b=BLK)
            nc.sync.dma_start(out=x_chunk[:], in_=rows[:, g * TILES : (g + 1) * TILES, :])
            return x_chunk

        def load_weight(words_tile, plane, words, scales):
            nc.sync.dma_start(
                out=words_tile[:].bitcast(I32), in_=words[0].rearrange("p n t -> p (n t)").bitcast(I32)
            )
            for quadrant in range(4):
                nc.sync.dma_start(
                    out=plane[32 * quadrant : 32 * quadrant + 4, :].bitcast(I32),
                    in_=scales[0, 4 * quadrant : 4 * quadrant + 4, :].bitcast(I32),
                )

        by_turns = [member * CHUNKS + g for g in range(CHUNKS) for member in range(PAIR)]
        x_order = by_turns + list(range(PAIR * CHUNKS, B * CHUNKS))
        x_chunks = {x_order[0]: load_x_chunk(x_order[0])}
        load_weight(k_words, k_plane, k_w_words, k_w_scales)
        load_weight(v_words, v_plane, v_w_words, v_w_scales)
        for index in x_order[1:X_BUFS]:
            x_chunks[index] = load_x_chunk(index)

        gain_bf = const.tile([P, NS * H], BF16)
        nc.scalar.dma_start(out=gain_bf[:], in_=scale_gain.rearrange("j h -> (j h)").partition_broadcast(P))
        vb_bf = const.tile([P, C], BF16)
        nc.scalar.dma_start(out=vb_bf[:], in_=v_b.partition_broadcast(P))
        kb_rows = const.tile([P, P], BF16)
        nc.vector.memset(kb_rows[:], 0.0)
        nc.scalar.dma_start(out=kb_rows[0:2, :], in_=k_b.rearrange("(r c) -> r c", r=2))

        identity_tile = const.tile([P, P], F32)
        make_identity(nc, identity_tile[:])
        identity = identity_tile[:]

        head_of = const.tile([P, 2], F32)
        nc.vector.memset(head_of[:], 0.0)
        for part in range(2):
            nc.vector.memset(head_of[part * HD : (part + 1) * HD, part : part + 1], 1.0)

        kb_f32 = const.tile([P, P], F32)
        nc.vector.tensor_copy(out=kb_f32[:], in_=kb_rows[:])
        kb_ps = psum.tile([P, P], F32, tag="f_ps")
        nc.tensor.transpose(out=kb_ps[:], in_=kb_f32[:], identity=identity)
        kb_col = const.tile([P, 2], F32)
        nc.vector.tensor_copy(out=kb_col[:], in_=kb_ps[:, 0:2])

        vb_bc = const.tile([P, H, HD], F32)
        nc.vector.tensor_copy(out=vb_bc[:], in_=vb_bf[:].rearrange("p (h c) -> p h c", h=H))

        gain = const.tile([P, H, NS], F32)
        nc.vector.tensor_copy(out=gain[:], in_=gain_bf[:].rearrange("p (j h) -> p h j", h=H))
        top = const.tile([P, H], F32)
        nc.vector.tensor_reduce(out=top[:], in_=gain[:], axis=mybir.AxisListType.X, op=ALU.max)
        nc.vector.tensor_tensor(
            out=gain[:], in0=gain[:], in1=top[:].unsqueeze(2).to_broadcast([P, H, NS]), op=ALU.subtract
        )
        nc.scalar.activation(out=gain[:], in_=gain[:], func=ACT.Exp)
        total = const.tile([P, H], F32)
        nc.vector.tensor_reduce(out=total[:], in_=gain[:], axis=mybir.AxisListType.X, op=ALU.add)
        nc.vector.reciprocal(out=total[:], in_=total[:])
        nc.vector.tensor_tensor(
            out=gain[:], in0=gain[:], in1=total[:].unsqueeze(2).to_broadcast([P, H, NS]), op=ALU.mult
        )
        coef_pow = const.tile([P, H, NS], F32)
        nc.vector.tensor_scalar_mul(out=coef_pow[:], in0=gain[:], scalar1=TAP2)
        nc.vector.scalar_tensor_tensor(
            out=coef_pow[:, :, 1:NS],
            in0=gain[:, :, 0 : NS - 1],
            scalar=TAP1,
            in1=coef_pow[:, :, 1:NS],
            op0=ALU.mult,
            op1=ALU.add,
        )
        coef_tri = const.tile([P, H, NS], F32)
        nc.vector.tensor_scalar_mul(out=coef_tri[:], in0=gain[:], scalar1=TAP0)

        shift_one = const.tile([P, P], F32)
        nc.vector.tensor_copy(out=shift_one[:, 1:P], in_=identity[:, 0 : P - 1])
        nc.vector.tensor_copy(out=shift_one[:, 0:1], in_=identity[:, P - 1 : P])
        not_last = const.tile([P, 1], F32)
        nc.vector.tensor_scalar(
            out=not_last[:], in0=identity[:, P - 1 : P], scalar1=-1.0, scalar2=1.0, op0=ALU.mult, op1=ALU.add
        )
        coef_pow_cut = const.tile([P, H, NS], F32)
        nc.vector.tensor_scalar_mul(out=coef_pow_cut[:], in0=coef_pow[:], scalar1=not_last[:, 0:1])
        coef_tri_cut = const.tile([P, H, NS], F32)
        nc.vector.tensor_scalar_mul(out=coef_tri_cut[:], in0=coef_tri[:], scalar1=not_last[:, 0:1])

        def coefs_of(h, shift):
            j = [j for j in range(NS) if shift in (2**j, 3 * 2**j)][0]
            whole, cut = (coef_pow, coef_pow_cut) if shift == 2**j else (coef_tri, coef_tri_cut)
            return whole[:, h, j : j + 1], cut[:, h, j : j + 1]

        def taps_of(h):
            taps = [(2**j, coef_pow[:, h, j : j + 1]) for j in range(NS)]
            taps += [(3 * 2**j, coef_tri[:, h, j : j + 1]) for j in range(NS)]
            return [tap for tap in taps if tap[0] < N]

        fields = [const.tile([P, BLK, H, PAIR, HD], F32, name="field%d" % pair, tag="field%d" % pair) for pair in range(B // PAIR)]
        norms = [const.tile([P, PAIR, BLK, H], F32, name="norm%d" % pair) for pair in range(B // PAIR)]

        quantised = {}

        def quantise_chunk(pair, chunk):
            x_chunk = x_chunks[pair * PAIR * CHUNKS + chunk]

            grouped = stage.tile([P, CHUNK, PACK], BF16, align_bytes=64, bufs=3)
            grouped_words = (
                grouped[:].rearrange("p n t -> p (n t)").bitcast(F32).rearrange("p (i a u) -> p i a u", i=TILES, u=2)
            )
            for j in range(TILES // 2):
                x_ps = psum.tile([P, 2, 2, P], F32, bufs=2)
                for t in range(2):
                    words = x_chunk[:, 2 * j + t, :].bitcast(F32)
                    for u in range(2):
                        nc.tensor.transpose(out=x_ps[:, t, u, :], in_=words[:, u : D // 2 : 2], identity=identity)
                nc.scalar.copy(
                    out=grouped_words[:, 2 * j : 2 * j + 2, :, :], in_=x_ps[:].rearrange("p t u a -> p t a u")
                )
            place = x_order.index(pair * PAIR * CHUNKS + chunk) + X_BUFS
            if place < len(x_order):
                x_chunks[x_order[place]] = load_x_chunk(x_order[place])
            x_codes = stage.tile([P, CHUNK], U32, align_bytes=64, bufs=PAIR * CHUNKS)
            x_plane = stage.tile([P, CHUNK], U8, align_bytes=64, bufs=PAIR * CHUNKS)
            quantised[(pair, chunk)] = (x_codes, x_plane)
            nc.vector.quantize_mx(
                out=x_codes[:].bitcast(FP8X4), scales=x_plane[:], in_=grouped[:].rearrange("p n t -> p (n t)")
            )

        def value_chunk(pair, chunk):
            member, g = divmod(chunk, CHUNKS)
            x_codes, x_plane = quantised[(pair, chunk)]
            for j in range(TILES // 2):
                v_ps = psum.tile([P, 2, H, HD], F32, bufs=2)
                for t in range(2):
                    cols = slice((2 * j + t) * P, (2 * j + t + 1) * P)
                    nc.tensor.matmul_mx(
                        out=v_ps[:, t, :, :].rearrange("p h c -> p (h c)"),
                        lhsT=x_codes[:, cols].bitcast(FP8X4),
                        lhsT_scale=x_plane[:, cols],
                        rhs=v_words[:].bitcast(FP8X4),
                        rhs_scale=v_plane[:],
                        start=True,
                        stop=True,
                    )
                b0 = g * TILES + 2 * j
                nc.vector.tensor_tensor(
                    out=fields[pair][:, b0 : b0 + 2, :, member, :],
                    in0=v_ps[:],
                    in1=vb_bc[:].unsqueeze(1).to_broadcast([P, 2, H, HD]),
                    op=ALU.add,
                )

        def norm_chunk(pair, chunk, half, now=()):
            member, g = divmod(chunk, CHUNKS)
            x_codes, x_plane = quantised[(pair, chunk)]
            cols = slice(half * P, (half + 1) * P)
            k_ps = psum.tile([P, CHUNK], F32)
            nc.tensor.matmul_mx(
                out=k_ps[:],
                lhsT=k_words[:, cols].bitcast(FP8X4),
                lhsT_scale=k_plane[:, cols],
                rhs=x_codes[:].bitcast(FP8X4),
                rhs_scale=x_plane[:],
                start=True,
                stop=True,
            )
            square = stage.tile([P, CHUNK], F32, bufs=3)
            nc.scalar.activation(out=square[:], in_=k_ps[:], func=ACT.Square, bias=kb_col[:, half : half + 1])
            m2_ps = psum.tile([P, TILES, 2], F32)
            for i in range(TILES):
                nc.tensor.matmul(
                    out=m2_ps[:, i, :], lhsT=square[:, i * P : (i + 1) * P], rhs=head_of[:], start=True, stop=True
                )
            nc.scalar.activation(
                out=norms[pair][:, member, g * TILES : (g + 1) * TILES, 2 * half : 2 * half + 2],
                in_=m2_ps[:],
                func=ACT.Sqrt,
            )
            for h in now:
                norm_by_scalar(pair, h, g, [member])

        toeplitz = const.tile([P, H, PITCH], F32)

        def build_toeplitz():
            diagonal = const.tile([P, H, PERIOD], F32)
            nc.gpsimd.memset(diagonal[:], 0.0)
            place = (0 - EARLY_A) % PERIOD
            nc.gpsimd.tensor_scalar(
                out=diagonal[:, :, place : place + 1],
                in0=coef_pow[:, :, 0:1],
                scalar1=0.0,
                scalar2=TAP3,
                op0=ALU.mult,
                op1=ALU.add,
            )
            for j in range(NS):
                for shift, coefs in ((2**j, coef_pow), (3 * 2**j, coef_tri)):
                    if shift % BLK == 0 and shift < N:
                        place = (shift // BLK - EARLY_A) % PERIOD
                        nc.gpsimd.tensor_copy(out=diagonal[:, :, place : place + 1], in_=coefs[:, :, j : j + 1])
            parked = out[0].rearrange("c n -> (c n)")
            nc.sync.dma_start(
                out=parked[0 : H * P * PERIOD].rearrange("(h r c) -> r h c", h=H, c=PERIOD), in_=diagonal[:]
            )
            for h in range(H):
                rows = parked[h * P * PERIOD : h * P * PERIOD + P * (PERIOD - 1)].rearrange("(r c) -> r c", c=PERIOD - 1)
                nc.sync.dma_start(out=toeplitz[:, h, 0:LATE_A], in_=rows[:, 0:LATE_A])

        def add_tap(acc, f_t, shift, coef, first, last):
            nc.vector.scalar_tensor_tensor(
                out=acc[:, first:last],
                in0=f_t[:, first - shift : last - shift],
                scalar=coef,
                in1=acc[:, first:last],
                op0=ALU.mult,
                op1=ALU.add,
            )

        def add_rows(acc_ab, f_ab, rows, coef, first, last, cols):
            nc.vector.scalar_tensor_tensor(
                out=acc_ab[:, first:last, cols],
                in0=f_ab[:, first - rows : last - rows, cols],
                scalar=coef,
                in1=acc_ab[:, first:last, cols],
                op0=ALU.mult,
                op1=ALU.add,
            )

        def group_adds(h, f_ab, acc_ab, g):
            cols = slice(g * TILES, (g + 1) * TILES)
            spans = [
                (shift // BLK, coef, first, last)
                for shift, coef in taps_of(h)
                if shift % BLK == 0
                for first, last in ((shift // BLK, P // 2), (max(shift // BLK, P // 2), P))
                if first < last
            ]
            return [lambda span=span: add_rows(acc_ab, f_ab, span[0], span[1], span[2], span[3], cols) for span in spans]

        def head_tiles():
            f_ab = work.tile([P, P, BLK], F32, bufs=3)
            acc_ab = work.tile([P, P, BLK], F32, bufs=4)
            return f_ab, acc_ab

        def norm_by_vector(pair, h, g):
            tiles = slice(g * TILES, (g + 1) * TILES)
            f = fields[pair][:, tiles, h, :, :]
            m = norms[pair][:, :, tiles, h : h + 1].rearrange("p m b o -> p b m o")
            nc.vector.tensor_tensor(out=f, in0=f, in1=m.to_broadcast([P, TILES, PAIR, HD]), op=ALU.mult)

        def norm_by_scalar(pair, h, g, members):
            for b in range(g * TILES, (g + 1) * TILES):
                for member in members:
                    nc.scalar.activation(
                        out=fields[pair][:, b, h, member, :],
                        in_=fields[pair][:, b, h, member, :],
                        func=ACT.Copy,
                        scale=norms[pair][:, member, b, h : h + 1],
                    )

        scaled_of = {}

        def scale_head(u):
            pair, h = heads[u]
            shifts = PE_SHIFTS.get(u, ())
            if shifts:
                if u % 2 == 0:
                    scaled = work.tile([P, len(shifts), BLK, PAIR * HD], F32, bufs=1)
                else:
                    scaled = const.tile([P, len(shifts), BLK, PAIR * HD], F32, tag="field0")
                scaled_of[u] = scaled
                for k, shift in enumerate(shifts):
                    whole, cut = coefs_of(h, shift)
                    pieces = [(first, first + TILES, whole) for first in range(0, BLK - TILES, TILES)]
                    pieces += [(BLK - TILES, BLK - shift, whole), (BLK - shift, BLK, cut)]
                    for first, last, coef in [piece for piece in pieces if piece[0] < piece[1]]:
                        nc.scalar.activation(
                            out=scaled[:, k, first:last, :],
                            in_=fields[pair][:, first:last, h, :, :].rearrange("p b m c -> p b (m c)"),
                            func=ACT.Copy,
                            scale=coef,
                        )

        def turn_group(u, g, filtered=True):
            pair, h = heads[u]
            f_ab, acc_ab = turned[u]
            shifts = PE_SHIFTS.get(u, ())
            scaled = scaled_of.get(u)
            late_ps = None
            if shifts:
                f_ps = psum.tile([P, TILES, P], F32, tag="v_ps", bufs=2)
                late_ps = psum.tile([P, TILES, P], F32, tag="x_ps", bufs=2)
            else:
                f_ps = psum.tile([P, TILES, P], F32)
                if filtered:
                    late_ps = psum.tile([P, TILES, P], F32)
            cols = slice(g * TILES, (g + 1) * TILES)
            for i in range(TILES):
                block = fields[pair][:, g * TILES + i, h, :, :].rearrange("p m c -> p (m c)")
                nc.tensor.transpose(out=f_ps[:, i, :], in_=block, identity=identity)
            nc.scalar.copy(out=f_ab[:, :, cols], in_=f_ps[:].rearrange("p i a -> p a i"))
            if not shifts:
                plain = EARLY_A if filtered else P
                nc.scalar.mul(out=acc_ab[:, 0:plain, cols], in_=f_ps[:, :, 0:plain].rearrange("p i a -> p a i"), mul=TAP3)
            for i in range(TILES):
                b = g * TILES + i
                block = fields[pair][:, b, h, :, :].rearrange("p m c -> p (m c)")
                for k, shift in enumerate(shifts):
                    nc.tensor.matmul(
                        out=late_ps[:, i, :],
                        lhsT=scaled[:, k, (b - shift) % BLK, :],
                        rhs=identity if b >= shift else shift_one[:],
                        start=k == 0,
                        stop=False,
                        is_transpose=True,
                    )
                if filtered:
                    nc.tensor.matmul(
                        out=late_ps[:, i, EARLY_A:P], lhsT=block, rhs=toeplitz[:, h, 0:LATE_A], start=not shifts, stop=True
                    )
            if shifts:
                nc.scalar.copy(out=acc_ab[:, :, cols], in_=late_ps[:].rearrange("p i a -> p a i"))
            elif filtered:
                nc.scalar.copy(out=acc_ab[:, EARLY_A:P, cols], in_=late_ps[:, :, EARLY_A:P].rearrange("p i a -> p a i"))

        def filter_head(pair, h, f_ab, acc_ab, beside, shifts=(), done_groups=0):
            f_t = f_ab[:].rearrange("p a b -> p (a b)")
            acc = acc_ab[:].rearrange("p a b -> p (a b)")

            taps = [tap for tap in taps_of(h) if tap[0] not in shifts]
            early = [tap for tap in taps if tap[0] < EARLY]
            if shifts:
                early = [(0, TAP3)] + early
            pieces = 3 if shifts else 2
            bounds = [EARLY + BLK * (LATE_A * i // pieces) for i in range(pieces + 1)]
            late = [(tap, i) for tap in taps if tap[0] % BLK != 0 for i in range(pieces)]
            slots = max(len(early), len(late))
            for k in range(slots):
                if k < len(early):
                    shift, coef = early[k]
                    if shift > 0 and shift % BLK == 0 and done_groups > 0:
                        add_rows(acc_ab, f_ab, shift // BLK, coef, shift // BLK, EARLY_A, slice(done_groups * TILES, BLK))
                    else:
                        add_tap(acc, f_t, shift, coef, shift, EARLY)
                if k < len(late):
                    (shift, coef), i = late[k]
                    add_tap(acc, f_t, shift, coef, bounds[i], bounds[i + 1])
                for task in beside[len(beside) * k // slots : len(beside) * (k + 1) // slots]:
                    task()
            for first, last in ((EARLY, EARLY + LATE_HALF), (EARLY + LATE_HALF, N), (0, EARLY)):
                for member in range(PAIR):
                    nc.sync.dma_start(
                        out=out[pair * PAIR + member, h * HD : (h + 1) * HD, first:last],
                        in_=acc[member * HD : (member + 1) * HD, first:last],
                    )

        def prepare_step(pair, order, step, fillers=(), now=()):
            thirds = [fillers[len(fillers) * i // 3 : len(fillers) * (i + 1) // 3] for i in range(3)]
            if step < len(order):
                quantise_chunk(pair, order[step])
            for task in thirds[0]:
                task()
            if step > 0:
                value_chunk(pair, order[step - 1])
            for task in thirds[1]:
                task()
            if step > 0:
                norm_chunk(pair, order[step - 1], 0, now)
            for task in thirds[2]:
                task()

        def second_halves(pair):
            return [lambda chunk=chunk: norm_chunk(pair, chunk, 1, (2,)) for chunk in range(PAIR * CHUNKS)]

        build_toeplitz()
        heads = [(pair, h) for pair in range(B // PAIR) for h in range(H)]
        turned = {0: head_tiles()}

        fillers = []
        for step in range(len(by_turns) + 1):
            prepare_step(0, by_turns, step)
            if step > 0 and step % PAIR == 0:
                g = step // PAIR - 1
                norm_by_vector(0, 0, g)
                turn_group(0, g, g >= BY_VECTOR)
                norm_by_scalar(0, 1, g, range(PAIR))
                if g < BY_VECTOR:
                    fillers.extend(group_adds(0, turned[0][0], turned[0][1], g))
        for task in fillers:
            task()

        in_order = list(range(PAIR * CHUNKS))
        steps = [lambda step=step: prepare_step(1, in_order, step, (), (0,)) for step in range(len(in_order) + 1)]
        beside = {
            0: second_halves(0),
            1: steps[0 : len(steps) // 2 + 1],
            LAST_STEPS: steps[len(steps) // 2 + 1 :],
            H - 1: second_halves(1),
        }
        def turn_task(u, g):
            turn_group(u, g)
            if u + 1 < len(heads) and heads[u + 1][1] % 2 == 1:
                norm_by_scalar(heads[u + 1][0], heads[u + 1][1], g, range(PAIR))

        scale_head(1)
        for u in range(len(heads)):
            tasks = beside.get(u, [])
            if u + 1 < len(heads):
                turned[u + 1] = head_tiles()
                turning = [lambda u=u, g=g: turn_task(u + 1, g) for g in range(CHUNKS)]
                if u == LAST_STEPS:
                    tasks = tasks + turning + [lambda u=u: scale_head(u + 2)]
                else:
                    for task in turning:
                        task()
            filter_head(
                heads[u][0], heads[u][1], turned[u][0], turned[u][1], tasks, PE_SHIFTS.get(u, ()),
                BY_VECTOR if u == 0 else 0,
            )
            if u + 2 < len(heads) and u != LAST_STEPS:
                scale_head(u + 2)
